import numpy as np
import ml_dtypes


def mxq(x, axis, fmt="e4m3"):
    dtype, down = {"e4m3": (ml_dtypes.float8_e4m3fn, 7), "e5m2": (ml_dtypes.float8_e5m2, 14)}[fmt]
    v = np.moveaxis(np.asarray(x, np.float32).astype(ml_dtypes.bfloat16).astype(np.float64), axis, -1)
    blocks = v.reshape(v.shape[:-1] + (-1, 32))
    amax = np.abs(blocks).max(-1, keepdims=True)
    byte = np.maximum(np.where(amax > 0, np.frexp(amax)[1] - 1 + 127, 0) - down, 1)
    scale = np.exp2(byte - 127.0)
    codes = (blocks / scale).astype(np.float32).astype(dtype).astype(np.float64)
    return np.moveaxis((codes * scale).reshape(v.shape), -1, axis)


WIDE = False


def mx_kscale(k):
    if not WIDE:
        return np.ones(k)
    levels = np.array([10, -10, 5, -5, 0])
    if k % 512:
        return np.exp2(np.random.permutation(np.resize(levels, k // 32))).repeat(32)
    a = np.empty((k // 512, 16))
    for p in range(k // 512):
        a[p, :8] = np.random.permutation(np.resize(levels, 8))
        for g in range(8):
            far = levels[np.abs(levels - a[p, g]) >= 10]
            a[p, g + 8] = far[np.random.randint(len(far))]
    return np.exp2(a.ravel()).repeat(32)


BF16 = ml_dtypes.bfloat16


def bf(x):
    return np.asarray(x, np.float32).astype(BF16)


def f64(x):
    return np.asarray(x).astype(np.float64)


B, G, D, H, DH, R, F, L = 1, 64, 512, 2, 256, 100, 4096, 2
S = G * G
INNER = H * DH
ROT = 2 * R
MAX_FREQ = 10.0
EPS = 1e-5


def make_freqs():
    exps = np.linspace(0.0, np.log(MAX_FREQ / 2.0) / np.log(2.0), R // 2)
    base = (2.0 ** exps) * np.pi
    t = np.linspace(-1.0, 1.0, G)
    f = np.repeat(t[:, None] * base[None, :], 2, axis=-1)
    fh = np.broadcast_to(f[:, None, :], (G, G, R))
    fw = np.broadcast_to(f[None, :, :], (G, G, R))
    return np.concatenate([fh, fw], axis=-1)


def rotate_half(u):
    u = u.reshape(u.shape[:-1] + (u.shape[-1] // 2, 2))
    return np.concatenate([-u[..., 1], u[..., 0]], axis=-1)


def apply_rot(t, cosf, sinf):
    tb = t.reshape(B, H, G, G, DH)
    tl, tr = tb[..., :ROT], tb[..., ROT:]
    tl = tl * cosf + rotate_half(tl) * sinf
    return np.concatenate([tl, tr], axis=-1).reshape(B, H, S, DH)


def to_heads(t):
    return t.reshape(B, S, H, DH).transpose(0, 2, 1, 3)


def setup_inputs():
    s = mx_kscale(D)
    return {'x_grid': bf(np.random.standard_normal((B, S, D))),
            'ln_g': bf((1.0 + 0.1 * np.random.standard_normal(D)) * s),
            'ln_b': bf(0.1 * np.random.standard_normal(D) * s),
            'w_qk': bf(np.random.standard_normal((D, 2 * INNER)) * 1.5 / np.sqrt(D) / s[:, None])}


def reference(x_grid, ln_g, ln_b, w_qk):
    x = f64(x_grid)
    mu = np.mean(x, axis=-1, keepdims=True)
    var = np.mean(np.square(x - mu), axis=-1, keepdims=True)
    xn = (x - mu) / np.sqrt(var + EPS) * f64(ln_g) + f64(ln_b)
    qk = mxq(xn, 2, 'e4m3') @ mxq(f64(w_qk), 0, 'e4m3')
    q, k = to_heads(qk[..., :INNER]), to_heads(qk[..., INNER:])
    freqs = make_freqs()
    cosf, sinf = np.cos(freqs)[None, None], np.sin(freqs)[None, None]
    return apply_rot(q, cosf, sinf), apply_rot(k, cosf, sinf)

@@ -1,0 +1,361 @@
+import math
+from contextlib import ExitStack
+
+import concourse.masks as masks
+import concourse.mybir as mybir
+
+F32 = mybir.dt.float32
+BF16 = mybir.dt.bfloat16
+I32 = mybir.dt.int32
+U32 = mybir.dt.uint32
+U8 = mybir.dt.uint8
+FP8X4 = mybir.dt.float8_e4m3fn_x4
+ALU = mybir.AluOpType
+ACT = mybir.ActivationFunctionType
+
+P = 128
+PACK = 4
+D = P * PACK
+TOKENS = 4096
+GRID = 64
+HEADS = 2
+DH = 256
+INNER = HEADS * DH
+ROT = 200
+HALF = ROT // 2
+FREQS = HALF // 2
+PLAIN = DH - ROT
+EPS = 1e-5
+
+BLOCKS = 4
+LANES = 8
+GROUP = 2
+GROUPS = BLOCKS * LANES // GROUP
+GROUP_TOKENS = GROUP * P
+SLOTS = BLOCKS + LANES
+
+FLOPS = 2 * TOKENS * D * 2 * INNER
+
+
+def rotary_turns(nc, work):
+    part = work.tile([P, 1], I32)
+    nc.gpsimd.iota(part[:], pattern=[[0, 1]], base=0, channel_multiplier=1)
+    offsets = work.tile([P, SLOTS], I32)
+    nc.gpsimd.iota(offsets[:, 0:BLOCKS], pattern=[[GRID // BLOCKS, BLOCKS]], base=0, channel_multiplier=0)
+    nc.gpsimd.iota(offsets[:, BLOCKS:SLOTS], pattern=[[1, LANES]], base=0, channel_multiplier=0)
+    row_base = work.tile([P, 1], I32)
+    nc.vector.tensor_single_scalar(out=row_base[:], in_=part[:], scalar=3, op=ALU.arith_shift_right)
+    col_base = work.tile([P, 1], I32)
+    nc.vector.tensor_scalar(
+        out=col_base[:], in0=part[:], scalar1=7, scalar2=3,
+        op0=ALU.bitwise_and, op1=ALU.logical_shift_left,
+    )
+    half_t = work.tile([P, SLOTS], F32)
+    nc.vector.tensor_scalar(
+        out=half_t[:, 0:BLOCKS], in0=offsets[:, 0:BLOCKS], scalar1=row_base[:, 0:1],
+        scalar2=1.0 / (GRID - 1), op0=ALU.add, op1=ALU.mult,
+    )
+    nc.vector.tensor_scalar(
+        out=half_t[:, BLOCKS:SLOTS], in0=offsets[:, BLOCKS:SLOTS], scalar1=col_base[:, 0:1],
+        scalar2=1.0 / (GRID - 1), op0=ALU.add, op1=ALU.mult,
+    )
+    nc.vector.tensor_scalar_add(out=half_t[:], in0=half_t[:], scalar1=-0.5)
+
+    beta = work.tile([P, FREQS], F32)
+    nc.vector.memset(beta[:, 0:1], 1.0)
+    ratio = 5.0 ** (1.0 / (FREQS - 1))
+    have = 1
+    while have < FREQS:
+        more = min(have, FREQS - have)
+        nc.vector.tensor_scalar_mul(
+            out=beta[:, have : have + more], in0=beta[:, 0:more], scalar1=ratio**have
+        )
+        have += more
+
+    shape = [P, SLOTS, FREQS]
+    turns = work.tile([P, 2, SLOTS, FREQS], F32)
+    nc.vector.tensor_tensor(
+        out=turns[:, 0], in0=half_t[:].unsqueeze(2).to_broadcast(shape),
+        in1=beta[:].unsqueeze(1).to_broadcast(shape), op=ALU.mult,
+    )
+    nc.vector.tensor_scalar_add(out=turns[:, 1], in0=turns[:, 0], scalar1=-0.25)
+    whole = work.tile([P, 2, SLOTS, FREQS], I32)
+    nc.vector.tensor_copy(out=whole[:], in_=turns[:])
+    rest = work.tile([P, 2, SLOTS, FREQS], F32)
+    nc.vector.tensor_tensor(out=rest[:], in0=turns[:], in1=whole[:], op=ALU.subtract)
+    return rest
+
+
+def rotary_tables(nc, keep, work, half_sin):
+    square = work.tile([P, 2, SLOTS, FREQS], F32)
+    nc.vector.tensor_tensor(out=square[:], in0=half_sin[:], in1=half_sin[:], op=ALU.mult)
+    cos_tab = keep.tile([P, SLOTS, HALF], F32)
+    sin_tab = keep.tile([P, SLOTS, HALF], F32)
+
+    def finish(table_slots, squares, sign):
+        count = squares.shape[1]
+        nc.vector.tensor_scalar(
+            out=table_slots.rearrange("p s (j e) -> p s j e", e=2),
+            in0=squares.unsqueeze(3).to_broadcast([P, count, FREQS, 2]),
+            scalar1=-2.0 * sign, scalar2=sign, op0=ALU.mult, op1=ALU.add,
+        )
+
+    finish(cos_tab[:], square[:, 0], 1.0)
+    finish(sin_tab[:, 0:LANES], square[:, 1, BLOCKS:SLOTS], 1.0)
+    finish(sin_tab[:, LANES:SLOTS], square[:, 1, 0:BLOCKS], -1.0)
+    return cos_tab, sin_tab
+
+
+def quantise_weights(nc, keep, work, raw):
+    cols = 2 * INNER
+    grouped = work.tile([P, cols, PACK], BF16, align_bytes=64)
+    nc.vector.tensor_copy(out=grouped[:], in_=raw[:].rearrange("p t n -> p n t"))
+    codes = keep.tile([P, cols], U32, align_bytes=64)
+    scales = keep.tile([P, cols], U8, align_bytes=64)
+    plain_grouped = work.tile([P, DH, PACK], BF16, align_bytes=64)
+    nc.vector.memset(plain_grouped[:], 0.0)
+    nc.vector.tensor_copy(
+        out=plain_grouped[:, 0 : 2 * HEADS * PLAIN, :].rearrange("p (g c) t -> p g c t", c=PLAIN),
+        in_=raw[:].rearrange("p t (g c) -> p g c t", c=DH)[:, :, ROT:DH, :],
+    )
+    nc.vector.quantize_mx(
+        out=codes[:].bitcast(FP8X4), scales=scales[:], in_=grouped[:].rearrange("p n t -> p (n t)")
+    )
+    plain_codes = keep.tile([P, DH], U32, align_bytes=64)
+    plain_scales = keep.tile([P, DH], U8, align_bytes=64)
+    nc.vector.quantize_mx(
+        out=plain_codes[:].bitcast(FP8X4), scales=plain_scales[:],
+        in_=plain_grouped[:].rearrange("p n t -> p (n t)"),
+    )
+    return codes, scales, plain_codes, plain_scales
+
+
+def tile_transformerencoderlayer_pa_t_kernel(tc, x_grid, ln_g, ln_b, w_qk, out_0, out_1):
+    nc = tc.nc
+    x_view = x_grid.rearrange("o (a p l) k -> p (o a) (l k)", a=BLOCKS, p=P, l=LANES)
+    out_views = [
+        out.rearrange("o h (a p l) c -> p (o h) a (l c)", a=BLOCKS, p=P, l=LANES)
+        for out in (out_0, out_1)
+    ]
+
+    with ExitStack() as ctx:
+        keep = ctx.enter_context(tc.tile_pool(name="keep", bufs=1))
+        work = ctx.enter_context(tc.tile_pool(name="work", bufs=1))
+        stats = ctx.enter_context(tc.tile_pool(name="stats", bufs=4))
+        stage = ctx.enter_context(tc.tile_pool(name="stage", bufs=3))
+        results = ctx.enter_context(tc.tile_pool(name="results", bufs=3))
+        zt_psum = ctx.enter_context(tc.psum_pool(name="zt_psum", bufs=2))
+        u_psum = ctx.enter_context(tc.psum_pool(name="u_psum", bufs=4))
+        plain_psum = ctx.enter_context(tc.psum_pool(name="plain_psum", bufs=2))
+        ctx.enter_context(tc.manual_schedule())
+
+        def block_and_lane(g):
+            return g // (LANES // GROUP), GROUP * (g % (LANES // GROUP))
+
+        x_sb = keep.tile([P, GROUPS, GROUP, D], BF16)
+
+        def load_x(g):
+            a, lane = block_and_lane(g)
+            nc.sync.dma_start(
+                out=x_sb[:, g].rearrange("p s k -> p (s k)"),
+                in_=x_view[:, a, lane * D : (lane + GROUP) * D],
+            )
+
+        gain_raw = work.tile([P, PACK], BF16)
+        bias_raw = work.tile([P, PACK], BF16)
+        w_raw = work.tile([P, PACK, 2 * INNER], BF16)
+        load_x(0)
+        nc.sync.dma_start(out=gain_raw[:], in_=ln_g.rearrange("(p t) -> p t", t=PACK))
+        nc.sync.dma_start(out=bias_raw[:], in_=ln_b.rearrange("(p t) -> p t", t=PACK))
+        load_x(1)
+        nc.sync.dma_start(out=w_raw[:], in_=w_qk.rearrange("(p t) n -> p t n", t=PACK))
+        for g in range(2, GROUPS):
+            load_x(g)
+
+        minus_half = keep.tile([P, GROUP], F32)
+        nc.vector.memset(minus_half[:], -0.5)
+        warm = work.tile([P, 1], F32)
+        nc.scalar.activation(out=warm[:], in_=minus_half[:, 0:1], func=ACT.Sin)
+        rest = rotary_turns(nc, work)
+        ident = keep.tile([P, P], F32)
+        masks.make_identity(nc, ident[:])
+        gain_bias = keep.tile([P, 2 * PACK], F32)
+        nc.vector.tensor_copy(out=gain_bias[:, 0:PACK], in_=gain_raw[:])
+        nc.vector.tensor_copy(out=gain_bias[:, PACK : 2 * PACK], in_=bias_raw[:])
+
+        discard = keep.tile([P, D], BF16)
+        neg_means, z_tiles, zt_banks, xn_grouped, xn_operands = {}, {}, {}, {}, {}
+        u_banks, plain_banks, y_tiles, partner_tiles = {}, {}, {}, {}
+
+        def sum_features(g):
+            total = stats.tile([P, GROUP], F32)
+            for s in range(GROUP):
+                nc.scalar.activation(
+                    out=discard[:], in_=x_sb[:, g, s], func=ACT.Copy, accum_out=total[:, s : s + 1]
+                )
+            neg_mean = stats.tile([P, GROUP], F32)
+            nc.gpsimd.tensor_scalar(
+                out=neg_mean[:], in0=total[:], scalar1=-1.0 / D, scalar2=0.0, op0=ALU.mult, op1=ALU.add
+            )
+            neg_means[g] = neg_mean
+
+        def normalise(g):
+            neg_mean = neg_means[g]
+            squares = stats.tile([P, GROUP], F32)
+            for s in range(GROUP):
+                nc.scalar.activation(
+                    out=discard[:], in_=x_sb[:, g, s], func=ACT.Square,
+                    bias=neg_mean[:, s : s + 1], accum_out=squares[:, s : s + 1],
+                )
+            var_eps = stats.tile([P, GROUP], F32)
+            nc.gpsimd.tensor_scalar(
+                out=var_eps[:], in0=squares[:], scalar1=1.0 / D, scalar2=EPS, op0=ALU.mult, op1=ALU.add
+            )
+            rstd = stats.tile([P, GROUP], F32)
+            nc.gpsimd.tensor_tensor(out=rstd[:], in0=var_eps[:], in1=minus_half[:], op=ALU.pow)
+            shift = stats.tile([P, GROUP], F32)
+            nc.gpsimd.tensor_tensor(out=shift[:], in0=neg_mean[:], in1=rstd[:], op=ALU.mult)
+            z = stage.tile([P, GROUP, D], F32)
+            for s in range(GROUP):
+                nc.gpsimd.tensor_scalar(
+                    out=z[:, s].rearrange("p (t m) -> p t m", t=PACK),
+                    in0=x_sb[:, g, s].rearrange("p (m t) -> p t m", t=PACK), scalar1=rstd[:, s : s + 1],
+                    scalar2=shift[:, s : s + 1], op0=ALU.mult, op1=ALU.add,
+                )
+            z_tiles[g] = z
+
+        def transpose(g):
+            z = z_tiles[g]
+            banks = []
+            for half in range(2):
+                zt = zt_psum.tile([P, 2, GROUP_TOKENS], F32, tag="zt")
+                for i in range(2):
+                    t = 2 * half + i
+                    for s in range(GROUP):
+                        nc.tensor.transpose(
+                            out=zt[:, i, s * P : (s + 1) * P], in_=z[:, s, t * P : (t + 1) * P],
+                            identity=ident[:],
+                        )
+                banks.append(zt)
+            zt_banks[g] = banks
+
+        def scale_shift_and_regroup(g):
+            planes = stage.tile([P, PACK, GROUP_TOKENS], BF16)
+            for half in range(2):
+                for i in range(2):
+                    t = 2 * half + i
+                    nc.scalar.activation(
+                        out=planes[:, t], in_=zt_banks[g][half][:, i], func=ACT.Identity,
+                        scale=gain_bias[:, t : t + 1], bias=gain_bias[:, PACK + t : PACK + t + 1],
+                    )
+            grouped = stage.tile([P, GROUP_TOKENS, PACK], BF16, align_bytes=64)
+            nc.scalar.copy(out=grouped[:], in_=planes[:].rearrange("p t w -> p w t"))
+            xn_grouped[g] = grouped
+
+        def quantise(g):
+            codes = stage.tile([P, GROUP_TOKENS], U32, align_bytes=64)
+            scales = stage.tile([P, GROUP_TOKENS], U8, align_bytes=64)
+            nc.vector.quantize_mx(
+                out=codes[:].bitcast(FP8X4), scales=scales[:],
+                in_=xn_grouped[g][:].rearrange("p w t -> p (w t)"),
+            )
+            xn_operands[g] = (codes, scales)
+
+        def project(g):
+            codes, scales = xn_operands[g]
+            for s in range(GROUP):
+                tokens = slice(s * P, (s + 1) * P)
+                for qk in range(2):
+                    columns = slice(qk * INNER, (qk + 1) * INNER)
+                    u = u_psum.tile([P, INNER], F32)
+                    nc.tensor.matmul_mx(
+                        out=u[:],
+                        lhsT=codes[:, tokens].bitcast(FP8X4), lhsT_scale=scales[:, tokens],
+                        rhs=w_codes[:, columns].bitcast(FP8X4), rhs_scale=w_scales[:, columns],
+                        start=True, stop=True,
+                    )
+                    u_banks[(g, s, qk)] = u
+            plain = plain_psum.tile([P, GROUP, DH], F32)
+            for s in range(GROUP):
+                tokens = slice(s * P, (s + 1) * P)
+                nc.tensor.matmul_mx(
+                    out=plain[:, s],
+                    lhsT=codes[:, tokens].bitcast(FP8X4), lhsT_scale=scales[:, tokens],
+                    rhs=plain_codes[:].bitcast(FP8X4), rhs_scale=plain_scales[:],
+                    start=True, stop=True,
+                )
+            plain_banks[g] = plain
+
+        def multiply_by_tables(g):
+            a, lane = block_and_lane(g)
+            y = results.tile([P, 2, HEADS, GROUP, DH], F32)
+            partner = results.tile([P, 2, HEADS, GROUP, ROT], F32)
+            both_heads = [P, HEADS, 2, HALF]
+            for s in range(GROUP):
+                l = lane + s
+                cosines = cos_tab[:, a : BLOCKS + l + 1 : BLOCKS + l - a]
+                sines = sin_tab[:, l : LANES + a + 1 : LANES + a - l]
+                for qk in range(2):
+                    u = u_banks[(g, s, qk)][:].rearrange("p (h c) -> p h c", h=HEADS)[:, :, 0:ROT]
+                    nc.vector.tensor_tensor(
+                        out=y[:, qk, :, s, 0:ROT].rearrange("p h (f c) -> p h f c", f=2),
+                        in0=u.rearrange("p h (f c) -> p h f c", f=2),
+                        in1=cosines.unsqueeze(1).to_broadcast(both_heads),
+                        op=ALU.mult,
+                    )
+                    nc.vector.tensor_tensor(
+                        out=partner[:, qk, :, s].rearrange("p h (e i) -> p h e i", e=2),
+                        in0=u.rearrange("p h (i e) -> p h e i", e=2),
+                        in1=sines.unsqueeze(1).to_broadcast(both_heads),
+                        op=ALU.mult,
+                    )
+            y_tiles[g] = y
+            partner_tiles[g] = partner
+
+        def add_and_store(g):
+            a, lane = block_and_lane(g)
+            y = y_tiles[g]
+            y_rows = y[:].rearrange("p q h s c -> p (q h s) c")
+            partner_rows = partner_tiles[g][:].rearrange("p q h s c -> p (q h s) c")
+            nc.vector.tensor_tensor(
+                out=y_rows[:, :, HALF:ROT], in0=y_rows[:, :, HALF:ROT],
+                in1=partner_rows[:, :, 0:HALF], op=ALU.add,
+            )
+            nc.vector.tensor_tensor(
+                out=y_rows[:, :, 0:HALF], in0=y_rows[:, :, 0:HALF],
+                in1=partner_rows[:, :, HALF:ROT], op=ALU.add,
+            )
+            nc.scalar.copy(
+                out=y[:].rearrange("p q h s c -> p s (q h) c")[:, :, :, ROT:DH],
+                in_=plain_banks[g][:, :, 0 : 2 * HEADS * PLAIN].rearrange("p s (g c) -> p s g c", c=PLAIN),
+            )
+            for qk in range(2):
+                nc.sync.dma_start(
+                    out=out_views[qk][:, :, a, lane * DH : (lane + GROUP) * DH],
+                    in_=y[:, qk].rearrange("p h s c -> p h (s c)"),
+                )
+
+        def exists(g):
+            return 0 <= g < GROUPS
+
+        for j in range(-2, GROUPS + 1):
+            if exists(j + 1):
+                normalise(j + 1)
+            if exists(j + 2):
+                sum_features(j + 2)
+            if j == -1:
+                half_sin = work.tile([P, 2, SLOTS, FREQS], F32)
+                nc.scalar.activation(out=half_sin[:], in_=rest[:], func=ACT.Sin, scale=math.pi)
+                w_codes, w_scales, plain_codes, plain_scales = quantise_weights(nc, keep, work, w_raw)
+                cos_tab, sin_tab = rotary_tables(nc, keep, work, half_sin)
+            if exists(j):
+                scale_shift_and_regroup(j)
+            if exists(j + 1):
+                transpose(j + 1)
+            if exists(j - 1):
+                multiply_by_tables(j - 1)
+            if exists(j):
+                quantise(j)
+                project(j)
+            if exists(j - 1):
+                add_and_store(j - 1)

@@ -32,6 +32,7 @@ LANES = 8
 GROUP = 2
 GROUPS = BLOCKS * LANES // GROUP
 GROUP_TOKENS = GROUP * P
+WHOLE = 4
 SLOTS = BLOCKS + LANES
 
 FLOPS = 2 * TOKENS * D * 2 * INNER
@@ -86,9 +87,7 @@ def rotary_turns(nc, work):
     return rest
 
 
-def rotary_tables(nc, keep, work, half_sin):
-    square = work.tile([P, 2, SLOTS, FREQS], F32)
-    nc.vector.tensor_tensor(out=square[:], in0=half_sin[:], in1=half_sin[:], op=ALU.mult)
+def rotary_tables(nc, keep, square):
     cos_tab = keep.tile([P, SLOTS, HALF], F32)
     sin_tab = keep.tile([P, SLOTS, HALF], F32)
 
@@ -106,28 +105,38 @@ def rotary_tables(nc, keep, work, half_sin):
     return cos_tab, sin_tab
 
 
-def quantise_weights(nc, keep, work, raw):
-    cols = 2 * INNER
-    grouped = work.tile([P, cols, PACK], BF16, align_bytes=64)
-    nc.vector.tensor_copy(out=grouped[:], in_=raw[:].rearrange("p t n -> p n t"))
-    codes = keep.tile([P, cols], U32, align_bytes=64)
-    scales = keep.tile([P, cols], U8, align_bytes=64)
-    plain_grouped = work.tile([P, DH, PACK], BF16, align_bytes=64)
-    nc.vector.memset(plain_grouped[:], 0.0)
+def regroup_weights(nc, work, raw, plain_grouped):
+    groupeds = []
+    for qk in range(2):
+        grouped = work.tile([P, INNER, PACK], BF16, align_bytes=64, tag="w_grouped%d" % qk)
+        nc.vector.tensor_copy(
+            out=grouped[:], in_=raw[:, :, qk * INNER : (qk + 1) * INNER].rearrange("p t n -> p n t")
+        )
+        groupeds.append(grouped)
     nc.vector.tensor_copy(
         out=plain_grouped[:, 0 : 2 * HEADS * PLAIN, :].rearrange("p (g c) t -> p g c t", c=PLAIN),
         in_=raw[:].rearrange("p t (g c) -> p g c t", c=DH)[:, :, ROT:DH, :],
     )
-    nc.vector.quantize_mx(
-        out=codes[:].bitcast(FP8X4), scales=scales[:], in_=grouped[:].rearrange("p n t -> p (n t)")
-    )
+    return groupeds
+
+
+def quantise_weights(nc, keep, groupeds, plain_grouped):
+    operands = []
+    for qk in range(2):
+        codes = keep.tile([P, INNER], U32, align_bytes=64, tag="w_codes%d" % qk)
+        scales = keep.tile([P, INNER], U8, align_bytes=64, tag="w_scales%d" % qk)
+        nc.vector.quantize_mx(
+            out=codes[:].bitcast(FP8X4), scales=scales[:],
+            in_=groupeds[qk][:].rearrange("p n t -> p (n t)"),
+        )
+        operands.append((codes, scales))
     plain_codes = keep.tile([P, DH], U32, align_bytes=64)
     plain_scales = keep.tile([P, DH], U8, align_bytes=64)
     nc.vector.quantize_mx(
         out=plain_codes[:].bitcast(FP8X4), scales=plain_scales[:],
         in_=plain_grouped[:].rearrange("p n t -> p (n t)"),
     )
-    return codes, scales, plain_codes, plain_scales
+    return operands, (plain_codes, plain_scales)
 
 
 def tile_transformerencoderlayer_pa_t_kernel(tc, x_grid, ln_g, ln_b, w_qk, out_0, out_1):
@@ -141,9 +150,9 @@ def tile_transformerencoderlayer_pa_t_kernel(tc, x_grid, ln_g, ln_b, w_qk, out_0
     with ExitStack() as ctx:
         keep = ctx.enter_context(tc.tile_pool(name="keep", bufs=1))
         work = ctx.enter_context(tc.tile_pool(name="work", bufs=1))
-        stats = ctx.enter_context(tc.tile_pool(name="stats", bufs=4))
+        stats = ctx.enter_context(tc.tile_pool(name="stats", bufs=6))
         stage = ctx.enter_context(tc.tile_pool(name="stage", bufs=3))
-        results = ctx.enter_context(tc.tile_pool(name="results", bufs=3))
+        results = ctx.enter_context(tc.tile_pool(name="results", bufs=4))
         zt_psum = ctx.enter_context(tc.psum_pool(name="zt_psum", bufs=2))
         u_psum = ctx.enter_context(tc.psum_pool(name="u_psum", bufs=4))
         plain_psum = ctx.enter_context(tc.psum_pool(name="plain_psum", bufs=2))
@@ -164,64 +173,109 @@ def tile_transformerencoderlayer_pa_t_kernel(tc, x_grid, ln_g, ln_b, w_qk, out_0
         gain_raw = work.tile([P, PACK], BF16)
         bias_raw = work.tile([P, PACK], BF16)
         w_raw = work.tile([P, PACK, 2 * INNER], BF16)
+        w_view = w_qk.rearrange("(p t) n -> p t n", t=PACK)
         load_x(0)
+        for qk in range(2):
+            columns = slice(qk * INNER, (qk + 1) * INNER)
+            nc.sync.dma_start(out=w_raw[:, :, columns], in_=w_view[:, :, columns])
+        load_x(1)
         nc.sync.dma_start(out=gain_raw[:], in_=ln_g.rearrange("(p t) -> p t", t=PACK))
         nc.sync.dma_start(out=bias_raw[:], in_=ln_b.rearrange("(p t) -> p t", t=PACK))
-        load_x(1)
-        nc.sync.dma_start(out=w_raw[:], in_=w_qk.rearrange("(p t) n -> p t n", t=PACK))
         for g in range(2, GROUPS):
             load_x(g)
 
-        minus_half = keep.tile([P, GROUP], F32)
+        minus_half = keep.tile([P, 2 * GROUP], F32)
         nc.vector.memset(minus_half[:], -0.5)
         warm = work.tile([P, 1], F32)
         nc.scalar.activation(out=warm[:], in_=minus_half[:, 0:1], func=ACT.Sin)
         rest = rotary_turns(nc, work)
         ident = keep.tile([P, P], F32)
         masks.make_identity(nc, ident[:])
-        gain_bias = keep.tile([P, 2 * PACK], F32)
-        nc.vector.tensor_copy(out=gain_bias[:, 0:PACK], in_=gain_raw[:])
-        nc.vector.tensor_copy(out=gain_bias[:, PACK : 2 * PACK], in_=bias_raw[:])
+        plain_grouped = work.tile([P, DH, PACK], BF16, align_bytes=64)
+        nc.gpsimd.memset(plain_grouped[:, 2 * HEADS * PLAIN : DH, :], 0.0)
+        half_sin = work.tile([P, 2, SLOTS, FREQS], F32)
+        nc.scalar.activation(out=half_sin[:], in_=rest[:], func=ACT.Sin, scale=math.pi)
+        square = work.tile([P, 2, SLOTS, FREQS], F32)
+        nc.scalar.activation(out=square[:], in_=half_sin[:], func=ACT.Square)
 
-        discard = keep.tile([P, D], BF16)
-        neg_means, z_tiles, zt_banks, xn_grouped, xn_operands = {}, {}, {}, {}, {}
+        discard_v = keep.tile([P, D], BF16)
+        discard_s = keep.tile([P, D], BF16)
+        neg_means, rstds, shifts = {}, {}, {}
+        square_sums = {}
+        z_tiles, zt_banks, plane_tiles, xn_grouped, xn_operands = {}, {}, {}, {}, {}
         u_banks, plain_banks, y_tiles, partner_tiles = {}, {}, {}, {}
 
-        def sum_features(g):
-            total = stats.tile([P, GROUP], F32)
-            for s in range(GROUP):
-                nc.scalar.activation(
-                    out=discard[:], in_=x_sb[:, g, s], func=ACT.Copy, accum_out=total[:, s : s + 1]
-                )
-            neg_mean = stats.tile([P, GROUP], F32)
+        def finish_statistics(owner, groups, variance_sums, scale):
+            count = GROUP * len(groups)
+            var_eps = stats.tile([P, 2 * GROUP], F32)
             nc.gpsimd.tensor_scalar(
-                out=neg_mean[:], in0=total[:], scalar1=-1.0 / D, scalar2=0.0, op0=ALU.mult, op1=ALU.add
+                out=var_eps[:, 0:count], in0=variance_sums, scalar1=scale, scalar2=EPS, op0=ALU.mult, op1=ALU.add
             )
-            neg_means[g] = neg_mean
+            rstd = stats.tile([P, 2 * GROUP], F32)
+            nc.gpsimd.tensor_tensor(
+                out=rstd[:, 0:count], in0=var_eps[:, 0:count], in1=minus_half[:, 0:count], op=ALU.pow
+            )
+            shift = stats.tile([P, 2 * GROUP], F32)
+            nc.gpsimd.tensor_tensor(
+                out=shift[:, 0:count], in0=owner[:, 0:count], in1=rstd[:, 0:count], op=ALU.mult
+            )
+            for n, g in enumerate(groups):
+                columns = slice(GROUP * n, GROUP * (n + 1))
+                neg_means[g] = owner[:, columns]
+                rstds[g] = rstd[:, columns]
+                shifts[g] = shift[:, columns]
+
+        def whole_statistics(g):
+            moments = stats.tile([P, GROUP, 2], F32)
+            for s in range(GROUP):
+                raw = stats.tile([P, 6], F32, tag="bn%d" % s)
+                nc.vector.bn_stats(out=raw[:], in_=x_sb[:, g, s])
+                nc.vector.bn_aggr(out=moments[:, s], in_=raw[:])
+            neg_mean = stats.tile([P, 2 * GROUP], F32)
+            nc.gpsimd.tensor_scalar(
+                out=neg_mean[:, 0:GROUP], in0=moments[:, :, 0], scalar1=-1.0, scalar2=0.0, op0=ALU.mult, op1=ALU.add
+            )
+            finish_statistics(neg_mean, [g], moments[:, :, 1], 1.0)
+
+        def average(g):
+            if g % 2 == 0:
+                neg_means[g] = stats.tile([P, 2 * GROUP], F32, name="neg_mean_pair")
+                square_sums[g] = stats.tile([P, 2 * GROUP], F32, name="square_sums")
+            first = g - g % 2
+            for s in range(GROUP):
+                column = GROUP * (g % 2) + s
+                nc.vector.tensor_scalar(
+                    out=discard_v[:], in0=x_sb[:, g, s], scalar1=-1.0 / D, scalar2=None,
+                    op0=ALU.mult, op1=ALU.add, accum_out=neg_means[first][:, column : column + 1],
+                )
+
+        def sum_squares(g):
+            first = g - g % 2
+            for s in range(GROUP):
+                column = GROUP * (g % 2) + s
+                nc.scalar.activation(
+                    out=discard_s[:], in_=x_sb[:, g, s], func=ACT.Square,
+                    bias=neg_means[first][:, column : column + 1],
+                    accum_out=square_sums[first][:, column : column + 1],
+                )
+            if g % 2 == 1:
+                finish_statistics(neg_means[first], [first, g], square_sums[first][:], 1.0 / D)
 
         def normalise(g):
-            neg_mean = neg_means[g]
-            squares = stats.tile([P, GROUP], F32)
-            for s in range(GROUP):
-                nc.scalar.activation(
-                    out=discard[:], in_=x_sb[:, g, s], func=ACT.Square,
-                    bias=neg_mean[:, s : s + 1], accum_out=squares[:, s : s + 1],
-                )
-            var_eps = stats.tile([P, GROUP], F32)
-            nc.gpsimd.tensor_scalar(
-                out=var_eps[:], in0=squares[:], scalar1=1.0 / D, scalar2=EPS, op0=ALU.mult, op1=ALU.add
-            )
-            rstd = stats.tile([P, GROUP], F32)
-            nc.gpsimd.tensor_tensor(out=rstd[:], in0=var_eps[:], in1=minus_half[:], op=ALU.pow)
-            shift = stats.tile([P, GROUP], F32)
-            nc.gpsimd.tensor_tensor(out=shift[:], in0=neg_mean[:], in1=rstd[:], op=ALU.mult)
             z = stage.tile([P, GROUP, D], F32)
             for s in range(GROUP):
-                nc.gpsimd.tensor_scalar(
-                    out=z[:, s].rearrange("p (t m) -> p t m", t=PACK),
-                    in0=x_sb[:, g, s].rearrange("p (m t) -> p t m", t=PACK), scalar1=rstd[:, s : s + 1],
-                    scalar2=shift[:, s : s + 1], op0=ALU.mult, op1=ALU.add,
-                )
+                out = z[:, s].rearrange("p (t m) -> p t m", t=PACK)
+                x = x_sb[:, g, s].rearrange("p (m t) -> p t m", t=PACK)
+                if s == 0:
+                    nc.gpsimd.tensor_scalar(
+                        out=out, in0=x, scalar1=rstds[g][:, s : s + 1],
+                        scalar2=shifts[g][:, s : s + 1], op0=ALU.mult, op1=ALU.add,
+                    )
+                else:
+                    nc.scalar.activation(
+                        out=out, in_=x, func=ACT.Identity,
+                        scale=rstds[g][:, s : s + 1], bias=shifts[g][:, s : s + 1],
+                    )
             z_tiles[g] = z
 
         def transpose(g):
@@ -239,17 +293,21 @@ def tile_transformerencoderlayer_pa_t_kernel(tc, x_grid, ln_g, ln_b, w_qk, out_0
                 banks.append(zt)
             zt_banks[g] = banks
 
-        def scale_shift_and_regroup(g):
+        def scale_and_shift(g):
             planes = stage.tile([P, PACK, GROUP_TOKENS], BF16)
-            for half in range(2):
-                for i in range(2):
-                    t = 2 * half + i
-                    nc.scalar.activation(
-                        out=planes[:, t], in_=zt_banks[g][half][:, i], func=ACT.Identity,
-                        scale=gain_bias[:, t : t + 1], bias=gain_bias[:, PACK + t : PACK + t + 1],
-                    )
+            for t in range(PACK):
+                nc.scalar.activation(
+                    out=planes[:, t], in_=zt_banks[g][t // 2][:, t % 2], func=ACT.Identity,
+                    scale=gain[:, t : t + 1], bias=bias[:, t : t + 1],
+                )
+            plane_tiles[g] = planes
+
+        def regroup(g):
             grouped = stage.tile([P, GROUP_TOKENS, PACK], BF16, align_bytes=64)
-            nc.scalar.copy(out=grouped[:], in_=planes[:].rearrange("p t w -> p w t"))
+            nc.scalar.copy(
+                out=grouped[:].rearrange("p (c i) t -> p c t i", i=4),
+                in_=plane_tiles[g][:].rearrange("p t (c i) -> p c t i", i=4),
+            )
             xn_grouped[g] = grouped
 
         def quantise(g):
@@ -261,101 +319,118 @@ def tile_transformerencoderlayer_pa_t_kernel(tc, x_grid, ln_g, ln_b, w_qk, out_0
             )
             xn_operands[g] = (codes, scales)
 
-        def project(g):
+        def project(g, s):
             codes, scales = xn_operands[g]
-            for s in range(GROUP):
-                tokens = slice(s * P, (s + 1) * P)
-                for qk in range(2):
-                    columns = slice(qk * INNER, (qk + 1) * INNER)
-                    u = u_psum.tile([P, INNER], F32)
-                    nc.tensor.matmul_mx(
-                        out=u[:],
-                        lhsT=codes[:, tokens].bitcast(FP8X4), lhsT_scale=scales[:, tokens],
-                        rhs=w_codes[:, columns].bitcast(FP8X4), rhs_scale=w_scales[:, columns],
-                        start=True, stop=True,
-                    )
-                    u_banks[(g, s, qk)] = u
-            plain = plain_psum.tile([P, GROUP, DH], F32)
-            for s in range(GROUP):
-                tokens = slice(s * P, (s + 1) * P)
+            tokens = slice(s * P, (s + 1) * P)
+            if s == 0:
+                plain_banks[g] = plain_psum.tile([P, GROUP, DH], F32, name="plain")
+            for qk in range(2):
+                u = u_psum.tile([P, INNER], F32)
                 nc.tensor.matmul_mx(
-                    out=plain[:, s],
+                    out=u[:],
                     lhsT=codes[:, tokens].bitcast(FP8X4), lhsT_scale=scales[:, tokens],
-                    rhs=plain_codes[:].bitcast(FP8X4), rhs_scale=plain_scales[:],
+                    rhs=w_operands[qk][0][:].bitcast(FP8X4), rhs_scale=w_operands[qk][1][:],
                     start=True, stop=True,
                 )
-            plain_banks[g] = plain
+                u_banks[(g, s, qk)] = u
+            nc.tensor.matmul_mx(
+                out=plain_banks[g][:, s],
+                lhsT=codes[:, tokens].bitcast(FP8X4), lhsT_scale=scales[:, tokens],
+                rhs=plain_operand[0][:].bitcast(FP8X4), rhs_scale=plain_operand[1][:],
+                start=True, stop=True,
+            )
 
-        def multiply_by_tables(g):
+        def multiply_by_tables(g, s):
             a, lane = block_and_lane(g)
-            y = results.tile([P, 2, HEADS, GROUP, DH], F32)
-            partner = results.tile([P, 2, HEADS, GROUP, ROT], F32)
+            if s == 0:
+                y_tiles[g] = results.tile([P, 2, HEADS, GROUP, DH], F32, name="y")
+                partner_tiles[g] = results.tile([P, 2, HEADS, GROUP, ROT], F32, name="partner")
+            y, partner = y_tiles[g], partner_tiles[g]
             both_heads = [P, HEADS, 2, HALF]
-            for s in range(GROUP):
-                l = lane + s
-                cosines = cos_tab[:, a : BLOCKS + l + 1 : BLOCKS + l - a]
-                sines = sin_tab[:, l : LANES + a + 1 : LANES + a - l]
-                for qk in range(2):
-                    u = u_banks[(g, s, qk)][:].rearrange("p (h c) -> p h c", h=HEADS)[:, :, 0:ROT]
-                    nc.vector.tensor_tensor(
-                        out=y[:, qk, :, s, 0:ROT].rearrange("p h (f c) -> p h f c", f=2),
-                        in0=u.rearrange("p h (f c) -> p h f c", f=2),
-                        in1=cosines.unsqueeze(1).to_broadcast(both_heads),
-                        op=ALU.mult,
-                    )
-                    nc.vector.tensor_tensor(
-                        out=partner[:, qk, :, s].rearrange("p h (e i) -> p h e i", e=2),
-                        in0=u.rearrange("p h (i e) -> p h e i", e=2),
-                        in1=sines.unsqueeze(1).to_broadcast(both_heads),
-                        op=ALU.mult,
-                    )
-            y_tiles[g] = y
-            partner_tiles[g] = partner
+            l = lane + s
+            cosines = cos_tab[:, a : BLOCKS + l + 1 : BLOCKS + l - a]
+            sines = sin_tab[:, l : LANES + a + 1 : LANES + a - l]
+            for qk in range(2):
+                u = u_banks[(g, s, qk)][:].rearrange("p (h c) -> p h c", h=HEADS)[:, :, 0:ROT]
+                nc.vector.tensor_tensor(
+                    out=y[:, qk, :, s, 0:ROT].rearrange("p h (f c) -> p h f c", f=2),
+                    in0=u.rearrange("p h (f c) -> p h f c", f=2),
+                    in1=cosines.unsqueeze(1).to_broadcast(both_heads),
+                    op=ALU.mult,
+                )
+                nc.vector.tensor_tensor(
+                    out=partner[:, qk, :, s].rearrange("p h (e i) -> p h e i", e=2),
+                    in0=u.rearrange("p h (i e) -> p h e i", e=2),
+                    in1=sines.unsqueeze(1).to_broadcast(both_heads),
+                    op=ALU.mult,
+                )
 
-        def add_and_store(g):
-            a, lane = block_and_lane(g)
-            y = y_tiles[g]
-            y_rows = y[:].rearrange("p q h s c -> p (q h s) c")
-            partner_rows = partner_tiles[g][:].rearrange("p q h s c -> p (q h s) c")
-            nc.vector.tensor_tensor(
-                out=y_rows[:, :, HALF:ROT], in0=y_rows[:, :, HALF:ROT],
-                in1=partner_rows[:, :, 0:HALF], op=ALU.add,
-            )
-            nc.vector.tensor_tensor(
-                out=y_rows[:, :, 0:HALF], in0=y_rows[:, :, 0:HALF],
-                in1=partner_rows[:, :, HALF:ROT], op=ALU.add,
-            )
+        def add(g, s):
+            engine = nc.vector if g == GROUPS - 1 else nc.gpsimd
+            y_rows = y_tiles[g][:, :, :, s].rearrange("p q h c -> p (q h) c")
+            partner_rows = partner_tiles[g][:, :, :, s].rearrange("p q h c -> p (q h) c")
+            for mine, other in ((slice(HALF, ROT), slice(0, HALF)), (slice(0, HALF), slice(HALF, ROT))):
+                engine.tensor_tensor(
+                    out=y_rows[:, :, mine], in0=y_rows[:, :, mine], in1=partner_rows[:, :, other], op=ALU.add
+                )
+
+        def copy_plain(g):
             nc.scalar.copy(
-                out=y[:].rearrange("p q h s c -> p s (q h) c")[:, :, :, ROT:DH],
+                out=y_tiles[g][:].rearrange("p q h s c -> p s (q h) c")[:, :, :, ROT:DH],
                 in_=plain_banks[g][:, :, 0 : 2 * HEADS * PLAIN].rearrange("p s (g c) -> p s g c", c=PLAIN),
             )
+
+        def store(g):
+            a, lane = block_and_lane(g)
             for qk in range(2):
                 nc.sync.dma_start(
                     out=out_views[qk][:, :, a, lane * DH : (lane + GROUP) * DH],
-                    in_=y[:, qk].rearrange("p h s c -> p h (s c)"),
+                    in_=y_tiles[g][:, qk].rearrange("p h s c -> p h (s c)"),
                 )
 
         def exists(g):
             return 0 <= g < GROUPS
 
+        whole_statistics(0)
+        normalise(0)
+        gain = keep.tile([P, PACK], F32)
+        nc.gpsimd.tensor_copy(out=gain[:], in_=gain_raw[:])
+        bias = keep.tile([P, PACK], F32)
+        nc.gpsimd.tensor_copy(out=bias[:], in_=bias_raw[:])
+        w_grouped = regroup_weights(nc, work, w_raw, plain_grouped)
+        whole_statistics(1)
+        w_operands, plain_operand = quantise_weights(nc, keep, w_grouped, plain_grouped)
+        whole_statistics(2)
+        cos_tab, sin_tab = rotary_tables(nc, keep, square)
+
         for j in range(-2, GROUPS + 1):
-            if exists(j + 1):
-                normalise(j + 1)
+            if exists(j - 1):
+                add(j - 1, 1)
+                store(j - 1)
             if exists(j + 2):
-                sum_features(j + 2)
-            if j == -1:
-                half_sin = work.tile([P, 2, SLOTS, FREQS], F32)
-                nc.scalar.activation(out=half_sin[:], in_=rest[:], func=ACT.Sin, scale=math.pi)
-                w_codes, w_scales, plain_codes, plain_scales = quantise_weights(nc, keep, work, w_raw)
-                cos_tab, sin_tab = rotary_tables(nc, keep, work, half_sin)
+                transpose(j + 2)
+                scale_and_shift(j + 2)
+            if exists(j + 3):
+                normalise(j + 3)
+            if exists(j + 2):
+                regroup(j + 2)
             if exists(j):
-                scale_shift_and_regroup(j)
+                multiply_by_tables(j, 0)
             if exists(j + 1):
-                transpose(j + 1)
-            if exists(j - 1):
-                multiply_by_tables(j - 1)
+                quantise(j + 1)
+                project(j + 1, 0)
             if exists(j):
-                quantise(j)
-                project(j)
-            if exists(j - 1):
-                add_and_store(j - 1)
+                multiply_by_tables(j, 1)
+                copy_plain(j)
+                add(j, 0)
+            if exists(j + 1):
+                project(j + 1, 1)
+            if j == -2:
+                whole_statistics(3)
+            if j == -1:
+                average(WHOLE)
+                average(WHOLE + 1)
+            if exists(j + 7) and j + 7 >= WHOLE + 2:
+                average(j + 7)
+            if exists(j + 5) and j + 5 >= WHOLE:
+                sum_squares(j + 5)

@@ -42,25 +42,26 @@ def rotary_turns(nc, work):
     part = work.tile([P, 1], I32)
     nc.gpsimd.iota(part[:], pattern=[[0, 1]], base=0, channel_multiplier=1)
     offsets = work.tile([P, SLOTS], I32)
-    nc.gpsimd.iota(offsets[:, 0:BLOCKS], pattern=[[GRID // BLOCKS, BLOCKS]], base=0, channel_multiplier=0)
-    nc.gpsimd.iota(offsets[:, BLOCKS:SLOTS], pattern=[[1, LANES]], base=0, channel_multiplier=0)
+    nc.gpsimd.iota(
+        offsets[:, 0:BLOCKS], pattern=[[2 * GRID // BLOCKS, BLOCKS]], base=1 - GRID, channel_multiplier=0
+    )
+    nc.gpsimd.iota(offsets[:, BLOCKS:SLOTS], pattern=[[2, LANES]], base=1 - GRID, channel_multiplier=0)
     row_base = work.tile([P, 1], I32)
-    nc.vector.tensor_single_scalar(out=row_base[:], in_=part[:], scalar=3, op=ALU.arith_shift_right)
+    nc.vector.tensor_scalar(
+        out=row_base[:], in0=part[:], scalar1=3, scalar2=1,
+        op0=ALU.arith_shift_right, op1=ALU.logical_shift_left,
+    )
     col_base = work.tile([P, 1], I32)
     nc.vector.tensor_scalar(
-        out=col_base[:], in0=part[:], scalar1=7, scalar2=3,
+        out=col_base[:], in0=part[:], scalar1=7, scalar2=4,
         op0=ALU.bitwise_and, op1=ALU.logical_shift_left,
     )
     half_t = work.tile([P, SLOTS], F32)
-    nc.vector.tensor_scalar(
-        out=half_t[:, 0:BLOCKS], in0=offsets[:, 0:BLOCKS], scalar1=row_base[:, 0:1],
-        scalar2=1.0 / (GRID - 1), op0=ALU.add, op1=ALU.mult,
-    )
-    nc.vector.tensor_scalar(
-        out=half_t[:, BLOCKS:SLOTS], in0=offsets[:, BLOCKS:SLOTS], scalar1=col_base[:, 0:1],
-        scalar2=1.0 / (GRID - 1), op0=ALU.add, op1=ALU.mult,
-    )
-    nc.vector.tensor_scalar_add(out=half_t[:], in0=half_t[:], scalar1=-0.5)
+    for slots, base in ((slice(0, BLOCKS), row_base), (slice(BLOCKS, SLOTS), col_base)):
+        nc.vector.tensor_scalar(
+            out=half_t[:, slots], in0=offsets[:, slots], scalar1=base[:, 0:1],
+            scalar2=0.5 / (GRID - 1), op0=ALU.add, op1=ALU.mult,
+        )
 
     beta = work.tile([P, FREQS], F32)
     nc.vector.memset(beta[:, 0:1], 1.0)
@@ -80,28 +81,28 @@ def rotary_turns(nc, work):
         in1=beta[:].unsqueeze(1).to_broadcast(shape), op=ALU.mult,
     )
     nc.vector.tensor_scalar_add(out=turns[:, 1], in0=turns[:, 0], scalar1=-0.25)
-    whole = work.tile([P, 2, SLOTS, FREQS], I32)
-    nc.vector.tensor_copy(out=whole[:], in_=turns[:])
-    rest = work.tile([P, 2, SLOTS, FREQS], F32)
-    nc.vector.tensor_tensor(out=rest[:], in0=turns[:], in1=whole[:], op=ALU.subtract)
-    return rest
+    return turns
 
 
-def rotary_tables(nc, keep, square):
+def rotary_tables(nc, keep, work, quarter_square):
+    product = work.tile([P, 2, SLOTS, FREQS], F32)
+    nc.vector.scalar_tensor_tensor(
+        out=product[:], in0=quarter_square[:], scalar=-1.0, in1=quarter_square[:], op0=ALU.add, op1=ALU.mult
+    )
     cos_tab = keep.tile([P, SLOTS, HALF], F32)
     sin_tab = keep.tile([P, SLOTS, HALF], F32)
 
-    def finish(table_slots, squares, sign):
-        count = squares.shape[1]
+    def finish(table_slots, products, sign):
+        count = products.shape[1]
         nc.vector.tensor_scalar(
             out=table_slots.rearrange("p s (j e) -> p s j e", e=2),
-            in0=squares.unsqueeze(3).to_broadcast([P, count, FREQS, 2]),
-            scalar1=-2.0 * sign, scalar2=sign, op0=ALU.mult, op1=ALU.add,
+            in0=products.unsqueeze(3).to_broadcast([P, count, FREQS, 2]),
+            scalar1=8.0 * sign, scalar2=sign, op0=ALU.mult, op1=ALU.add,
         )
 
-    finish(cos_tab[:], square[:, 0], 1.0)
-    finish(sin_tab[:, 0:LANES], square[:, 1, BLOCKS:SLOTS], 1.0)
-    finish(sin_tab[:, LANES:SLOTS], square[:, 1, 0:BLOCKS], -1.0)
+    finish(cos_tab[:], product[:, 0], 1.0)
+    finish(sin_tab[:, 0:BLOCKS], product[:, 1, 0:BLOCKS], -1.0)
+    finish(sin_tab[:, BLOCKS:SLOTS], product[:, 1, BLOCKS:SLOTS], 1.0)
     return cos_tab, sin_tab
 
 
@@ -184,89 +185,95 @@ def tile_transformerencoderlayer_pa_t_kernel(tc, x_grid, ln_g, ln_b, w_qk, out_0
         for g in range(2, GROUPS):
             load_x(g)
 
-        minus_half = keep.tile([P, 2 * GROUP], F32)
+        minus_half = keep.tile([P, GROUP], F32)
         nc.vector.memset(minus_half[:], -0.5)
+        eps = keep.tile([P, 1], F32)
+        nc.vector.tensor_scalar(
+            out=eps[:], in0=minus_half[:, 0:1], scalar1=0.0, scalar2=EPS, op0=ALU.mult, op1=ALU.add
+        )
         warm = work.tile([P, 1], F32)
         nc.scalar.activation(out=warm[:], in_=minus_half[:, 0:1], func=ACT.Sin)
-        rest = rotary_turns(nc, work)
+        turns = rotary_turns(nc, work)
         ident = keep.tile([P, P], F32)
         masks.make_identity(nc, ident[:])
         plain_grouped = work.tile([P, DH, PACK], BF16, align_bytes=64)
         nc.gpsimd.memset(plain_grouped[:, 2 * HEADS * PLAIN : DH, :], 0.0)
-        half_sin = work.tile([P, 2, SLOTS, FREQS], F32)
-        nc.scalar.activation(out=half_sin[:], in_=rest[:], func=ACT.Sin, scale=math.pi)
-        square = work.tile([P, 2, SLOTS, FREQS], F32)
-        nc.scalar.activation(out=square[:], in_=half_sin[:], func=ACT.Square)
+        eighth_sin = work.tile([P, 2, SLOTS, FREQS], F32)
+        eighth_square = work.tile([P, 2, SLOTS, FREQS], F32)
+        quarter_square = work.tile([P, 2, SLOTS, FREQS], F32)
 
         discard_v = keep.tile([P, D], BF16)
         discard_s = keep.tile([P, D], BF16)
-        neg_means, rstds, shifts = {}, {}, {}
-        square_sums = {}
+        means, variances, unfinished, rstds, shifts = {}, {}, {}, {}, {}
         z_tiles, zt_banks, plane_tiles, xn_grouped, xn_operands = {}, {}, {}, {}, {}
         u_banks, plain_banks, y_tiles, partner_tiles = {}, {}, {}, {}
 
-        def finish_statistics(owner, groups, variance_sums, scale):
-            count = GROUP * len(groups)
-            var_eps = stats.tile([P, 2 * GROUP], F32)
-            nc.gpsimd.tensor_scalar(
-                out=var_eps[:, 0:count], in0=variance_sums, scalar1=scale, scalar2=EPS, op0=ALU.mult, op1=ALU.add
+        def finish_statistics(g, rstd):
+            shift = stats.tile([P, GROUP], F32)
+            mean, sign = means[g]
+            nc.vector.scalar_tensor_tensor(
+                out=shift[:], in0=mean, scalar=sign, in1=rstd[:], op0=ALU.mult, op1=ALU.mult
             )
-            rstd = stats.tile([P, 2 * GROUP], F32)
-            nc.gpsimd.tensor_tensor(
-                out=rstd[:, 0:count], in0=var_eps[:, 0:count], in1=minus_half[:, 0:count], op=ALU.pow
-            )
-            shift = stats.tile([P, 2 * GROUP], F32)
-            nc.gpsimd.tensor_tensor(
-                out=shift[:, 0:count], in0=owner[:, 0:count], in1=rstd[:, 0:count], op=ALU.mult
-            )
-            for n, g in enumerate(groups):
-                columns = slice(GROUP * n, GROUP * (n + 1))
-                neg_means[g] = owner[:, columns]
-                rstds[g] = rstd[:, columns]
-                shifts[g] = shift[:, columns]
+            rstds[g], shifts[g] = rstd, shift
 
-        def whole_statistics(g):
+        def measure_whole(g):
             moments = stats.tile([P, GROUP, 2], F32)
             for s in range(GROUP):
                 raw = stats.tile([P, 6], F32, tag="bn%d" % s)
                 nc.vector.bn_stats(out=raw[:], in_=x_sb[:, g, s])
                 nc.vector.bn_aggr(out=moments[:, s], in_=raw[:])
-            neg_mean = stats.tile([P, 2 * GROUP], F32)
-            nc.gpsimd.tensor_scalar(
-                out=neg_mean[:, 0:GROUP], in0=moments[:, :, 0], scalar1=-1.0, scalar2=0.0, op0=ALU.mult, op1=ALU.add
-            )
-            finish_statistics(neg_mean, [g], moments[:, :, 1], 1.0)
+            means[g] = (moments[:, :, 0], -1.0)
+            variances[g] = (moments[:, :, 1], 1.0)
 
         def average(g):
-            if g % 2 == 0:
-                neg_means[g] = stats.tile([P, 2 * GROUP], F32, name="neg_mean_pair")
-                square_sums[g] = stats.tile([P, 2 * GROUP], F32, name="square_sums")
-            first = g - g % 2
+            neg_mean = stats.tile([P, GROUP], F32)
             for s in range(GROUP):
-                column = GROUP * (g % 2) + s
                 nc.vector.tensor_scalar(
                     out=discard_v[:], in0=x_sb[:, g, s], scalar1=-1.0 / D, scalar2=None,
-                    op0=ALU.mult, op1=ALU.add, accum_out=neg_means[first][:, column : column + 1],
+                    op0=ALU.mult, op1=ALU.add, accum_out=neg_mean[:, s : s + 1],
                 )
+            means[g] = (neg_mean[:], 1.0)
 
         def sum_squares(g):
-            first = g - g % 2
+            squares = stats.tile([P, GROUP], F32)
             for s in range(GROUP):
-                column = GROUP * (g % 2) + s
                 nc.scalar.activation(
                     out=discard_s[:], in_=x_sb[:, g, s], func=ACT.Square,
-                    bias=neg_means[first][:, column : column + 1],
-                    accum_out=square_sums[first][:, column : column + 1],
+                    bias=means[g][0][:, s : s + 1], accum_out=squares[:, s : s + 1],
                 )
-            if g % 2 == 1:
-                finish_statistics(neg_means[first], [first, g], square_sums[first][:], 1.0 / D)
+            variances[g] = (squares[:], 1.0 / D)
+
+        def power_rstd(g):
+            variance, scale = variances[g]
+            var_eps = stats.tile([P, GROUP], F32)
+            nc.gpsimd.tensor_scalar(
+                out=var_eps[:], in0=variance, scalar1=scale, scalar2=EPS, op0=ALU.mult, op1=ALU.add
+            )
+            rstd = stats.tile([P, GROUP], F32, name="rstd_g")
+            nc.gpsimd.tensor_tensor(out=rstd[:], in0=var_eps[:], in1=minus_half[:], op=ALU.pow)
+            mean, sign = means[g]
+            neg_mean = stats.tile([P, GROUP], F32, name="neg_mean_g")
+            nc.gpsimd.tensor_scalar(
+                out=neg_mean[:], in0=mean, scalar1=sign, scalar2=0.0, op0=ALU.mult, op1=ALU.add
+            )
+            shift = stats.tile([P, GROUP], F32, name="shift_g")
+            nc.gpsimd.tensor_tensor(out=shift[:], in0=neg_mean[:], in1=rstd[:], op=ALU.mult)
+            rstds[g], shifts[g] = rstd, shift
+
+        def table_rstd(g):
+            variance, scale = variances[g]
+            rstd = stats.tile([P, GROUP], F32, name="rstd_s")
+            nc.scalar.activation(
+                out=rstd[:], in_=variance, func=ACT.Abs_reciprocal_sqrt, scale=scale, bias=eps[:]
+            )
+            unfinished[g] = rstd
 
         def normalise(g):
             z = stage.tile([P, GROUP, D], F32)
             for s in range(GROUP):
                 out = z[:, s].rearrange("p (t m) -> p t m", t=PACK)
                 x = x_sb[:, g, s].rearrange("p (m t) -> p t m", t=PACK)
-                if s == 0:
+                if g < 2 and s == 0:
                     nc.gpsimd.tensor_scalar(
                         out=out, in0=x, scalar1=rstds[g][:, s : s + 1],
                         scalar2=shifts[g][:, s : s + 1], op0=ALU.mult, op1=ALU.add,
@@ -340,39 +347,34 @@ def tile_transformerencoderlayer_pa_t_kernel(tc, x_grid, ln_g, ln_b, w_qk, out_0
                 start=True, stop=True,
             )
 
-        def multiply_by_tables(g, s):
+        def multiply_by_tables(g, s, qk):
             a, lane = block_and_lane(g)
-            if s == 0:
+            if s == 0 and qk == 0:
                 y_tiles[g] = results.tile([P, 2, HEADS, GROUP, DH], F32, name="y")
                 partner_tiles[g] = results.tile([P, 2, HEADS, GROUP, ROT], F32, name="partner")
-            y, partner = y_tiles[g], partner_tiles[g]
             both_heads = [P, HEADS, 2, HALF]
             l = lane + s
-            cosines = cos_tab[:, a : BLOCKS + l + 1 : BLOCKS + l - a]
-            sines = sin_tab[:, l : LANES + a + 1 : LANES + a - l]
-            for qk in range(2):
-                u = u_banks[(g, s, qk)][:].rearrange("p (h c) -> p h c", h=HEADS)[:, :, 0:ROT]
-                nc.vector.tensor_tensor(
-                    out=y[:, qk, :, s, 0:ROT].rearrange("p h (f c) -> p h f c", f=2),
-                    in0=u.rearrange("p h (f c) -> p h f c", f=2),
-                    in1=cosines.unsqueeze(1).to_broadcast(both_heads),
-                    op=ALU.mult,
-                )
-                nc.vector.tensor_tensor(
-                    out=partner[:, qk, :, s].rearrange("p h (e i) -> p h e i", e=2),
-                    in0=u.rearrange("p h (i e) -> p h e i", e=2),
-                    in1=sines.unsqueeze(1).to_broadcast(both_heads),
-                    op=ALU.mult,
-                )
+            slots = slice(a, BLOCKS + l + 1, BLOCKS + l - a)
+            u = u_banks[(g, s, qk)][:].rearrange("p (h c) -> p h c", h=HEADS)[:, :, 0:ROT]
+            nc.vector.tensor_tensor(
+                out=y_tiles[g][:, qk, :, s, 0:ROT].rearrange("p h (f c) -> p h f c", f=2),
+                in0=u.rearrange("p h (f c) -> p h f c", f=2),
+                in1=cos_tab[:, slots].unsqueeze(1).to_broadcast(both_heads),
+                op=ALU.mult,
+            )
+            nc.vector.tensor_tensor(
+                out=partner_tiles[g][:, qk, :, s].rearrange("p h (f i) -> p h f i", f=2),
+                in0=u.rearrange("p h (i e) -> p h e i", e=2)[:, :, ::-1, :],
+                in1=sin_tab[:, slots].unsqueeze(1).to_broadcast(both_heads),
+                op=ALU.mult,
+            )
 
         def add(g, s):
-            engine = nc.vector if g == GROUPS - 1 else nc.gpsimd
-            y_rows = y_tiles[g][:, :, :, s].rearrange("p q h c -> p (q h) c")
-            partner_rows = partner_tiles[g][:, :, :, s].rearrange("p q h c -> p (q h) c")
-            for mine, other in ((slice(HALF, ROT), slice(0, HALF)), (slice(0, HALF), slice(HALF, ROT))):
-                engine.tensor_tensor(
-                    out=y_rows[:, :, mine], in0=y_rows[:, :, mine], in1=partner_rows[:, :, other], op=ALU.add
-                )
+            engine = nc.vector if (g, s) == (GROUPS - 1, GROUP - 1) else nc.gpsimd
+            rows = y_tiles[g][:, :, :, s, 0:ROT].rearrange("p q h c -> p (q h) c")
+            engine.tensor_tensor(
+                out=rows, in0=rows, in1=partner_tiles[g][:, :, :, s].rearrange("p q h c -> p (q h) c"), op=ALU.add
+            )
 
         def copy_plain(g):
             nc.scalar.copy(
@@ -391,46 +393,64 @@ def tile_transformerencoderlayer_pa_t_kernel(tc, x_grid, ln_g, ln_b, w_qk, out_0
         def exists(g):
             return 0 <= g < GROUPS
 
-        whole_statistics(0)
+        measure_whole(0)
+        nc.scalar.activation(out=eighth_sin[:], in_=turns[:], func=ACT.Sin, scale=math.pi / 4)
+        nc.scalar.activation(out=eighth_square[:], in_=eighth_sin[:], func=ACT.Square)
+        power_rstd(0)
         normalise(0)
+        nc.scalar.activation(out=quarter_square[:], in_=eighth_square[:], func=ACT.Square, scale=-2.0, bias=1.0)
         gain = keep.tile([P, PACK], F32)
         nc.gpsimd.tensor_copy(out=gain[:], in_=gain_raw[:])
         bias = keep.tile([P, PACK], F32)
         nc.gpsimd.tensor_copy(out=bias[:], in_=bias_raw[:])
         w_grouped = regroup_weights(nc, work, w_raw, plain_grouped)
-        whole_statistics(1)
+        measure_whole(1)
+        power_rstd(1)
         w_operands, plain_operand = quantise_weights(nc, keep, w_grouped, plain_grouped)
-        whole_statistics(2)
-        cos_tab, sin_tab = rotary_tables(nc, keep, square)
 
         for j in range(-2, GROUPS + 1):
             if exists(j - 1):
                 add(j - 1, 1)
-                store(j - 1)
+            if exists(j + 3) and j + 3 >= WHOLE:
+                table_rstd(j + 3)
             if exists(j + 2):
                 transpose(j + 2)
                 scale_and_shift(j + 2)
-            if exists(j + 3):
-                normalise(j + 3)
+            if exists(j - 1):
+                copy_plain(j - 1)
+                store(j - 1)
             if exists(j + 2):
                 regroup(j + 2)
             if exists(j):
-                multiply_by_tables(j, 0)
+                multiply_by_tables(j, 0, 0)
+            if j == -2:
+                measure_whole(2)
+                power_rstd(2)
+                cos_tab, sin_tab = rotary_tables(nc, keep, work, quarter_square)
             if exists(j + 1):
                 quantise(j + 1)
+            if exists(j + 4):
+                if j + 4 < WHOLE:
+                    if j + 4 == WHOLE - 1:
+                        measure_whole(j + 4)
+                        power_rstd(j + 4)
+                elif j % 2 == 0:
+                    average(j + 4)
+                else:
+                    measure_whole(j + 4)
+            if exists(j):
+                multiply_by_tables(j, 0, 1)
+            if exists(j + 3) and j + 3 >= WHOLE:
+                finish_statistics(j + 3, unfinished[j + 3])
+            if exists(j + 3):
+                normalise(j + 3)
+            if exists(j + 1):
                 project(j + 1, 0)
             if exists(j):
-                multiply_by_tables(j, 1)
-                copy_plain(j)
+                multiply_by_tables(j, 1, 0)
+                multiply_by_tables(j, 1, 1)
                 add(j, 0)
             if exists(j + 1):
                 project(j + 1, 1)
-            if j == -2:
-                whole_statistics(3)
-            if j == -1:
-                average(WHOLE)
-                average(WHOLE + 1)
-            if exists(j + 7) and j + 7 >= WHOLE + 2:
-                average(j + 7)
-            if exists(j + 5) and j + 5 >= WHOLE:
-                sum_squares(j + 5)
+            if exists(j + 4) and j + 4 >= WHOLE and j % 2 == 0:
+                sum_squares(j + 4)

@@ -211,9 +211,11 @@ def tile_transformerencoderlayer_pa_t_kernel(tc, x_grid, ln_g, ln_b, w_qk, out_0
         def finish_statistics(g, rstd):
             shift = stats.tile([P, GROUP], F32)
             mean, sign = means[g]
-            nc.vector.scalar_tensor_tensor(
-                out=shift[:], in0=mean, scalar=sign, in1=rstd[:], op0=ALU.mult, op1=ALU.mult
-            )
+            for s in range(GROUP):
+                nc.vector.tensor_scalar(
+                    out=shift[:, s : s + 1], in0=mean[:, s : s + 1], scalar1=rstd[:, s : s + 1], scalar2=sign,
+                    op0=ALU.mult, op1=ALU.mult,
+                )
             rstds[g], shifts[g] = rstd, shift
 
         def measure_whole(g):
@@ -421,14 +423,14 @@ def tile_transformerencoderlayer_pa_t_kernel(tc, x_grid, ln_g, ln_b, w_qk, out_0
                 store(j - 1)
             if exists(j + 2):
                 regroup(j + 2)
-            if exists(j):
-                multiply_by_tables(j, 0, 0)
             if j == -2:
                 measure_whole(2)
                 power_rstd(2)
                 cos_tab, sin_tab = rotary_tables(nc, keep, work, quarter_square)
-            if exists(j + 1):
-                quantise(j + 1)
+            if exists(j):
+                multiply_by_tables(j, 0, 0)
+                multiply_by_tables(j, 0, 1)
+                add(j, 0)
             if exists(j + 4):
                 if j + 4 < WHOLE:
                     if j + 4 == WHOLE - 1:
@@ -438,19 +440,18 @@ def tile_transformerencoderlayer_pa_t_kernel(tc, x_grid, ln_g, ln_b, w_qk, out_0
                     average(j + 4)
                 else:
                     measure_whole(j + 4)
-            if exists(j):
-                multiply_by_tables(j, 0, 1)
             if exists(j + 3) and j + 3 >= WHOLE:
                 finish_statistics(j + 3, unfinished[j + 3])
             if exists(j + 3):
                 normalise(j + 3)
-            if exists(j + 1):
-                project(j + 1, 0)
             if exists(j):
                 multiply_by_tables(j, 1, 0)
-                multiply_by_tables(j, 1, 1)
-                add(j, 0)
             if exists(j + 1):
+                quantise(j + 1)
+            if exists(j):
+                multiply_by_tables(j, 1, 1)
+            if exists(j + 1):
+                project(j + 1, 0)
                 project(j + 1, 1)
             if exists(j + 4) and j + 4 >= WHOLE and j % 2 == 0:
                 sum_squares(j + 4)

@@ -38,7 +38,7 @@ SLOTS = BLOCKS + LANES
 FLOPS = 2 * TOKENS * D * 2 * INNER
 
 
-def rotary_turns(nc, work):
+def rotary_factors(nc, work):
     part = work.tile([P, 1], I32)
     nc.gpsimd.iota(part[:], pattern=[[0, 1]], base=0, channel_multiplier=1)
     offsets = work.tile([P, SLOTS], I32)
@@ -63,24 +63,29 @@ def rotary_turns(nc, work):
             scalar2=0.5 / (GRID - 1), op0=ALU.add, op1=ALU.mult,
         )
 
-    beta = work.tile([P, FREQS], F32)
-    nc.vector.memset(beta[:, 0:1], 1.0)
     ratio = 5.0 ** (1.0 / (FREQS - 1))
-    have = 1
-    while have < FREQS:
-        more = min(have, FREQS - have)
-        nc.vector.tensor_scalar_mul(
-            out=beta[:, have : have + more], in0=beta[:, 0:more], scalar1=ratio**have
-        )
-        have += more
-
-    shape = [P, SLOTS, FREQS]
-    turns = work.tile([P, 2, SLOTS, FREQS], F32)
+    rows = work.tile([P, 2, 8], F32)
+    nc.vector.memset(rows[:, :, 0:1], 1.0)
+    for have in (1, 2, 4):
+        for row, step in ((0, 8), (1, 1)):
+            nc.vector.tensor_scalar_mul(
+                out=rows[:, row, have : 2 * have], in0=rows[:, row, 0:have], scalar1=ratio ** (step * have)
+            )
+    beta = work.tile([P, 8, 8], F32)
     nc.vector.tensor_tensor(
-        out=turns[:, 0], in0=half_t[:].unsqueeze(2).to_broadcast(shape),
-        in1=beta[:].unsqueeze(1).to_broadcast(shape), op=ALU.mult,
+        out=beta[:], in0=rows[:, 0].unsqueeze(2).to_broadcast([P, 8, 8]),
+        in1=rows[:, 1].unsqueeze(1).to_broadcast([P, 8, 8]), op=ALU.mult,
     )
-    nc.vector.tensor_scalar_add(out=turns[:, 1], in0=turns[:, 0], scalar1=-0.25)
+    return half_t, beta[:].rearrange("p i j -> p (i j)")[:, 0:FREQS]
+
+
+def rotary_turns(nc, work, half_t, beta):
+    shape = [P, SLOTS, FREQS]
+    turns = work.tile([P, SLOTS, FREQS], F32)
+    nc.vector.tensor_tensor(
+        out=turns[:], in0=half_t[:].unsqueeze(2).to_broadcast(shape),
+        in1=beta.unsqueeze(1).to_broadcast(shape), op=ALU.mult,
+    )
     return turns
 
 
@@ -114,10 +119,12 @@ def regroup_weights(nc, work, raw, plain_grouped):
             out=grouped[:], in_=raw[:, :, qk * INNER : (qk + 1) * INNER].rearrange("p t n -> p n t")
         )
         groupeds.append(grouped)
-    nc.vector.tensor_copy(
-        out=plain_grouped[:, 0 : 2 * HEADS * PLAIN, :].rearrange("p (g c) t -> p g c t", c=PLAIN),
-        in_=raw[:].rearrange("p t (g c) -> p g c t", c=DH)[:, :, ROT:DH, :],
-    )
+    for head in range(2 * HEADS):
+        nc.gpsimd.tensor_scalar(
+            out=plain_grouped[:, head * PLAIN : (head + 1) * PLAIN, :],
+            in0=raw[:, :, head * DH + ROT : (head + 1) * DH].rearrange("p t n -> p n t"),
+            scalar1=1.0, scalar2=0.0, op0=ALU.mult, op1=ALU.add,
+        )
     return groupeds
 
 
@@ -191,9 +198,15 @@ def tile_transformerencoderlayer_pa_t_kernel(tc, x_grid, ln_g, ln_b, w_qk, out_0
         nc.vector.tensor_scalar(
             out=eps[:], in0=minus_half[:, 0:1], scalar1=0.0, scalar2=EPS, op0=ALU.mult, op1=ALU.add
         )
+        quarter_back = keep.tile([P, 2], F32)
+        for quarter in range(2):
+            nc.vector.tensor_scalar(
+                out=quarter_back[:, quarter : quarter + 1], in0=minus_half[:, 0:1],
+                scalar1=quarter * math.pi / 8, scalar2=0.0, op0=ALU.mult, op1=ALU.add,
+            )
         warm = work.tile([P, 1], F32)
         nc.scalar.activation(out=warm[:], in_=minus_half[:, 0:1], func=ACT.Sin)
-        turns = rotary_turns(nc, work)
+        half_t, beta = rotary_factors(nc, work)
         ident = keep.tile([P, P], F32)
         masks.make_identity(nc, ident[:])
         plain_grouped = work.tile([P, DH, PACK], BF16, align_bytes=64)
@@ -396,10 +409,16 @@ def tile_transformerencoderlayer_pa_t_kernel(tc, x_grid, ln_g, ln_b, w_qk, out_0
             return 0 <= g < GROUPS
 
         measure_whole(0)
-        nc.scalar.activation(out=eighth_sin[:], in_=turns[:], func=ACT.Sin, scale=math.pi / 4)
+        turns = rotary_turns(nc, work, half_t, beta)
+        for quarter in range(2):
+            nc.scalar.activation(
+                out=eighth_sin[:, quarter], in_=turns[:], func=ACT.Sin,
+                scale=math.pi / 4, bias=quarter_back[:, quarter : quarter + 1],
+            )
         nc.scalar.activation(out=eighth_square[:], in_=eighth_sin[:], func=ACT.Square)
         power_rstd(0)
         normalise(0)
+        transpose(0)
         nc.scalar.activation(out=quarter_square[:], in_=eighth_square[:], func=ACT.Square, scale=-2.0, bias=1.0)
         gain = keep.tile([P, PACK], F32)
         nc.gpsimd.tensor_copy(out=gain[:], in_=gain_raw[:])
@@ -409,49 +428,57 @@ def tile_transformerencoderlayer_pa_t_kernel(tc, x_grid, ln_g, ln_b, w_qk, out_0
         measure_whole(1)
         power_rstd(1)
         w_operands, plain_operand = quantise_weights(nc, keep, w_grouped, plain_grouped)
+        cos_tab, sin_tab = rotary_tables(nc, keep, work, quarter_square)
+
+        def take_statistics(g):
+            if g < WHOLE:
+                measure_whole(g)
+                power_rstd(g)
+            elif g % 2 == 0:
+                average(g)
+            else:
+                measure_whole(g)
 
         for j in range(-2, GROUPS + 1):
+            first, later = j + 2, j + 3
             if exists(j - 1):
                 add(j - 1, 1)
-            if exists(j + 3) and j + 3 >= WHOLE:
-                table_rstd(j + 3)
-            if exists(j + 2):
-                transpose(j + 2)
-                scale_and_shift(j + 2)
+            if exists(j + 5) and j >= 0:
+                take_statistics(j + 5)
+            if exists(later) and j >= 0:
+                normalise(later)
+            if exists(first):
+                scale_and_shift(first)
             if exists(j - 1):
                 copy_plain(j - 1)
                 store(j - 1)
-            if exists(j + 2):
-                regroup(j + 2)
+            if exists(first):
+                regroup(first)
+            if exists(later) and j < 0:
+                normalise(later)
             if j == -2:
-                measure_whole(2)
-                power_rstd(2)
-                cos_tab, sin_tab = rotary_tables(nc, keep, work, quarter_square)
+                nc.scalar.activation(out=warm[:], in_=eps[:], func=ACT.Abs_reciprocal_sqrt)
+                take_statistics(2)
             if exists(j):
                 multiply_by_tables(j, 0, 0)
                 multiply_by_tables(j, 0, 1)
-                add(j, 0)
-            if exists(j + 4):
-                if j + 4 < WHOLE:
-                    if j + 4 == WHOLE - 1:
-                        measure_whole(j + 4)
-                        power_rstd(j + 4)
-                elif j % 2 == 0:
-                    average(j + 4)
-                else:
-                    measure_whole(j + 4)
-            if exists(j + 3) and j + 3 >= WHOLE:
-                finish_statistics(j + 3, unfinished[j + 3])
-            if exists(j + 3):
-                normalise(j + 3)
-            if exists(j):
-                multiply_by_tables(j, 1, 0)
             if exists(j + 1):
                 quantise(j + 1)
+            if j == -1:
+                take_statistics(3)
+                take_statistics(4)
+            if exists(j + 4) and j + 4 >= WHOLE and j >= 0:
+                finish_statistics(j + 4, unfinished[j + 4])
             if exists(j):
+                add(j, 0)
+                multiply_by_tables(j, 1, 0)
                 multiply_by_tables(j, 1, 1)
+            if exists(later):
+                transpose(later)
             if exists(j + 1):
                 project(j + 1, 0)
                 project(j + 1, 1)
-            if exists(j + 4) and j + 4 >= WHOLE and j % 2 == 0:
-                sum_squares(j + 4)
+            if exists(j + 5) and j + 5 >= WHOLE:
+                if j % 2 == 1:
+                    sum_squares(j + 5)
+                table_rstd(j + 5)

@@ -111,21 +111,22 @@ def rotary_tables(nc, keep, work, quarter_square):
     return cos_tab, sin_tab
 
 
-def regroup_weights(nc, work, raw, plain_grouped):
+def regroup_weights(nc, work, raw):
     groupeds = []
-    for qk in range(2):
+    for qk, copy in ((0, nc.scalar.copy), (1, nc.vector.tensor_copy)):
         grouped = work.tile([P, INNER, PACK], BF16, align_bytes=64, tag="w_grouped%d" % qk)
-        nc.vector.tensor_copy(
-            out=grouped[:], in_=raw[:, :, qk * INNER : (qk + 1) * INNER].rearrange("p t n -> p n t")
-        )
+        copy(out=grouped[:], in_=raw[:, :, qk * INNER : (qk + 1) * INNER].rearrange("p t n -> p n t"))
         groupeds.append(grouped)
+    return groupeds
+
+
+def regroup_plain(nc, raw, plain_grouped):
     for head in range(2 * HEADS):
         nc.gpsimd.tensor_scalar(
             out=plain_grouped[:, head * PLAIN : (head + 1) * PLAIN, :],
             in0=raw[:, :, head * DH + ROT : (head + 1) * DH].rearrange("p t n -> p n t"),
             scalar1=1.0, scalar2=0.0, op0=ALU.mult, op1=ALU.add,
         )
-    return groupeds
 
 
 def quantise_weights(nc, keep, groupeds, plain_grouped):
@@ -215,21 +216,20 @@ def tile_transformerencoderlayer_pa_t_kernel(tc, x_grid, ln_g, ln_b, w_qk, out_0
         eighth_square = work.tile([P, 2, SLOTS, FREQS], F32)
         quarter_square = work.tile([P, 2, SLOTS, FREQS], F32)
 
-        discard_v = keep.tile([P, D], BF16)
-        discard_s = keep.tile([P, D], BF16)
-        means, variances, unfinished, rstds, shifts = {}, {}, {}, {}, {}
+        discard = keep.tile([P, D], BF16)
+        means, variances, rstds, shifts = {}, {}, {}, {}
         z_tiles, zt_banks, plane_tiles, xn_grouped, xn_operands = {}, {}, {}, {}, {}
         u_banks, plain_banks, y_tiles, partner_tiles = {}, {}, {}, {}
 
-        def finish_statistics(g, rstd):
+        def finish_statistics(g):
             shift = stats.tile([P, GROUP], F32)
-            mean, sign = means[g]
             for s in range(GROUP):
+                mean, sign = means[(g, s)]
                 nc.vector.tensor_scalar(
-                    out=shift[:, s : s + 1], in0=mean[:, s : s + 1], scalar1=rstd[:, s : s + 1], scalar2=sign,
+                    out=shift[:, s : s + 1], in0=mean, scalar1=rstds[g][s], scalar2=sign,
                     op0=ALU.mult, op1=ALU.mult,
                 )
-            rstds[g], shifts[g] = rstd, shift
+            shifts[g] = [shift[:, s : s + 1] for s in range(GROUP)]
 
         def measure_whole(g):
             moments = stats.tile([P, GROUP, 2], F32)
@@ -237,68 +237,67 @@ def tile_transformerencoderlayer_pa_t_kernel(tc, x_grid, ln_g, ln_b, w_qk, out_0
                 raw = stats.tile([P, 6], F32, tag="bn%d" % s)
                 nc.vector.bn_stats(out=raw[:], in_=x_sb[:, g, s])
                 nc.vector.bn_aggr(out=moments[:, s], in_=raw[:])
-            means[g] = (moments[:, :, 0], -1.0)
-            variances[g] = (moments[:, :, 1], 1.0)
+            means[g], variances[g] = moments[:, :, 0], moments[:, :, 1]
 
-        def average(g):
-            neg_mean = stats.tile([P, GROUP], F32)
-            for s in range(GROUP):
-                nc.vector.tensor_scalar(
-                    out=discard_v[:], in0=x_sb[:, g, s], scalar1=-1.0 / D, scalar2=None,
-                    op0=ALU.mult, op1=ALU.add, accum_out=neg_mean[:, s : s + 1],
-                )
-            means[g] = (neg_mean[:], 1.0)
+        def measure_first(g):
+            moments = stats.tile([P, 2], F32, name="first_moments")
+            raw = stats.tile([P, 6], F32, tag="bn0")
+            nc.vector.bn_stats(out=raw[:], in_=x_sb[:, g, 0])
+            nc.vector.bn_aggr(out=moments[:], in_=raw[:])
+            means[(g, 0)] = (moments[:, 0:1], -1.0)
+            variances[(g, 0)] = (moments[:, 1:2], 1.0)
 
-        def sum_squares(g):
-            squares = stats.tile([P, GROUP], F32)
+        def average_second(g):
+            neg_mean = stats.tile([P, 1], F32)
+            nc.scalar.activation(
+                out=discard[:], in_=x_sb[:, g, 1], func=ACT.Copy, scale=-1.0 / D, accum_out=neg_mean[:]
+            )
+            means[(g, 1)] = (neg_mean[:], 1.0)
+
+        def square_second(g):
+            squares = stats.tile([P, 1], F32)
+            nc.scalar.activation(
+                out=discard[:], in_=x_sb[:, g, 1], func=ACT.Square, bias=means[(g, 1)][0], accum_out=squares[:]
+            )
+            variances[(g, 1)] = (squares[:], 1.0 / D)
+
+        def table_rstd(g):
+            rstd = stats.tile([P, GROUP], F32, name="rstd_s")
             for s in range(GROUP):
+                variance, scale = variances[(g, s)]
                 nc.scalar.activation(
-                    out=discard_s[:], in_=x_sb[:, g, s], func=ACT.Square,
-                    bias=means[g][0][:, s : s + 1], accum_out=squares[:, s : s + 1],
+                    out=rstd[:, s : s + 1], in_=variance, func=ACT.Abs_reciprocal_sqrt, scale=scale, bias=eps[:]
                 )
-            variances[g] = (squares[:], 1.0 / D)
+            rstds[g] = [rstd[:, s : s + 1] for s in range(GROUP)]
 
         def power_rstd(g):
-            variance, scale = variances[g]
+            mean, variance = means[g], variances[g]
             var_eps = stats.tile([P, GROUP], F32)
             nc.gpsimd.tensor_scalar(
-                out=var_eps[:], in0=variance, scalar1=scale, scalar2=EPS, op0=ALU.mult, op1=ALU.add
+                out=var_eps[:], in0=variance, scalar1=1.0, scalar2=EPS, op0=ALU.mult, op1=ALU.add
             )
             rstd = stats.tile([P, GROUP], F32, name="rstd_g")
             nc.gpsimd.tensor_tensor(out=rstd[:], in0=var_eps[:], in1=minus_half[:], op=ALU.pow)
-            mean, sign = means[g]
             neg_mean = stats.tile([P, GROUP], F32, name="neg_mean_g")
             nc.gpsimd.tensor_scalar(
-                out=neg_mean[:], in0=mean, scalar1=sign, scalar2=0.0, op0=ALU.mult, op1=ALU.add
+                out=neg_mean[:], in0=mean, scalar1=-1.0, scalar2=0.0, op0=ALU.mult, op1=ALU.add
             )
             shift = stats.tile([P, GROUP], F32, name="shift_g")
             nc.gpsimd.tensor_tensor(out=shift[:], in0=neg_mean[:], in1=rstd[:], op=ALU.mult)
-            rstds[g], shifts[g] = rstd, shift
+            rstds[g] = [rstd[:, s : s + 1] for s in range(GROUP)]
+            shifts[g] = [shift[:, s : s + 1] for s in range(GROUP)]
 
-        def table_rstd(g):
-            variance, scale = variances[g]
-            rstd = stats.tile([P, GROUP], F32, name="rstd_s")
-            nc.scalar.activation(
-                out=rstd[:], in_=variance, func=ACT.Abs_reciprocal_sqrt, scale=scale, bias=eps[:]
-            )
-            unfinished[g] = rstd
-
-        def normalise(g):
-            z = stage.tile([P, GROUP, D], F32)
-            for s in range(GROUP):
-                out = z[:, s].rearrange("p (t m) -> p t m", t=PACK)
-                x = x_sb[:, g, s].rearrange("p (m t) -> p t m", t=PACK)
-                if g < 2 and s == 0:
-                    nc.gpsimd.tensor_scalar(
-                        out=out, in0=x, scalar1=rstds[g][:, s : s + 1],
-                        scalar2=shifts[g][:, s : s + 1], op0=ALU.mult, op1=ALU.add,
-                    )
-                else:
-                    nc.scalar.activation(
-                        out=out, in_=x, func=ACT.Identity,
-                        scale=rstds[g][:, s : s + 1], bias=shifts[g][:, s : s + 1],
-                    )
-            z_tiles[g] = z
+        def normalise(g, s):
+            if g not in z_tiles:
+                z_tiles[g] = stage.tile([P, GROUP, D], F32, name="z")
+            out = z_tiles[g][:, s].rearrange("p (t m) -> p t m", t=PACK)
+            x = x_sb[:, g, s].rearrange("p (m t) -> p t m", t=PACK)
+            if s == 0:
+                nc.gpsimd.tensor_scalar(
+                    out=out, in0=x, scalar1=rstds[g][s], scalar2=shifts[g][s], op0=ALU.mult, op1=ALU.add
+                )
+            else:
+                nc.scalar.activation(out=out, in_=x, func=ACT.Identity, scale=rstds[g][s], bias=shifts[g][s])
 
         def transpose(g):
             z = z_tiles[g]
@@ -385,7 +384,7 @@ def tile_transformerencoderlayer_pa_t_kernel(tc, x_grid, ln_g, ln_b, w_qk, out_0
             )
 
         def add(g, s):
-            engine = nc.vector if (g, s) == (GROUPS - 1, GROUP - 1) else nc.gpsimd
+            engine = nc.vector if s == GROUP - 1 and g >= GROUPS - 2 else nc.gpsimd
             rows = y_tiles[g][:, :, :, s, 0:ROT].rearrange("p q h c -> p (q h) c")
             engine.tensor_tensor(
                 out=rows, in0=rows, in1=partner_tiles[g][:, :, :, s].rearrange("p q h c -> p (q h) c"), op=ALU.add
@@ -410,6 +409,7 @@ def tile_transformerencoderlayer_pa_t_kernel(tc, x_grid, ln_g, ln_b, w_qk, out_0
 
         measure_whole(0)
         turns = rotary_turns(nc, work, half_t, beta)
+        w_grouped = regroup_weights(nc, work, w_raw)
         for quarter in range(2):
             nc.scalar.activation(
                 out=eighth_sin[:, quarter], in_=turns[:], func=ACT.Sin,
@@ -417,68 +417,71 @@ def tile_transformerencoderlayer_pa_t_kernel(tc, x_grid, ln_g, ln_b, w_qk, out_0
             )
         nc.scalar.activation(out=eighth_square[:], in_=eighth_sin[:], func=ACT.Square)
         power_rstd(0)
-        normalise(0)
+        normalise(0, 0)
+        normalise(0, 1)
         transpose(0)
         nc.scalar.activation(out=quarter_square[:], in_=eighth_square[:], func=ACT.Square, scale=-2.0, bias=1.0)
         gain = keep.tile([P, PACK], F32)
         nc.gpsimd.tensor_copy(out=gain[:], in_=gain_raw[:])
         bias = keep.tile([P, PACK], F32)
         nc.gpsimd.tensor_copy(out=bias[:], in_=bias_raw[:])
-        w_grouped = regroup_weights(nc, work, w_raw, plain_grouped)
+        regroup_plain(nc, w_raw, plain_grouped)
         measure_whole(1)
         power_rstd(1)
         w_operands, plain_operand = quantise_weights(nc, keep, w_grouped, plain_grouped)
         cos_tab, sin_tab = rotary_tables(nc, keep, work, quarter_square)
 
-        def take_statistics(g):
-            if g < WHOLE:
-                measure_whole(g)
-                power_rstd(g)
-            elif g % 2 == 0:
-                average(g)
-            else:
-                measure_whole(g)
-
         for j in range(-2, GROUPS + 1):
             first, later = j + 2, j + 3
+            new = j + 5
+            fresh = exists(new) and new >= WHOLE
             if exists(j - 1):
                 add(j - 1, 1)
-            if exists(j + 5) and j >= 0:
-                take_statistics(j + 5)
+            if fresh and j >= 0:
+                measure_first(new)
             if exists(later) and j >= 0:
-                normalise(later)
+                normalise(later, 1)
             if exists(first):
                 scale_and_shift(first)
+            if fresh:
+                average_second(new)
             if exists(j - 1):
                 copy_plain(j - 1)
                 store(j - 1)
             if exists(first):
                 regroup(first)
             if exists(later) and j < 0:
-                normalise(later)
+                normalise(later, 0)
+                normalise(later, 1)
             if j == -2:
                 nc.scalar.activation(out=warm[:], in_=eps[:], func=ACT.Abs_reciprocal_sqrt)
-                take_statistics(2)
+                measure_whole(2)
+                power_rstd(2)
             if exists(j):
                 multiply_by_tables(j, 0, 0)
                 multiply_by_tables(j, 0, 1)
             if exists(j + 1):
                 quantise(j + 1)
             if j == -1:
-                take_statistics(3)
-                take_statistics(4)
+                measure_whole(3)
+                power_rstd(3)
+                measure_first(new)
             if exists(j + 4) and j + 4 >= WHOLE and j >= 0:
-                finish_statistics(j + 4, unfinished[j + 4])
+                finish_statistics(j + 4)
             if exists(j):
                 add(j, 0)
+            if exists(j + 4) and j >= -1:
+                normalise(j + 4, 0)
+            if exists(j):
                 multiply_by_tables(j, 1, 0)
                 multiply_by_tables(j, 1, 1)
-            if exists(later):
+            if exists(later) and j >= 0:
                 transpose(later)
             if exists(j + 1):
                 project(j + 1, 0)
                 project(j + 1, 1)
-            if exists(j + 5) and j + 5 >= WHOLE:
-                if j % 2 == 1:
-                    sum_squares(j + 5)
-                table_rstd(j + 5)
+            if exists(later) and j < 0:
+                transpose(later)
+            if fresh:
+                square_second(new)
+                table_rstd(new)

@@ -25,6 +25,7 @@ ROT = 200
 HALF = ROT // 2
 FREQS = HALF // 2
 PLAIN = DH - ROT
+WINDOW = 64
 EPS = 1e-5
 
 BLOCKS = 4
@@ -32,6 +33,7 @@ LANES = 8
 GROUP = 2
 GROUPS = BLOCKS * LANES // GROUP
 GROUP_TOKENS = GROUP * P
+LATE = 12
 WHOLE = 4
 SLOTS = BLOCKS + LANES
 
@@ -97,55 +99,39 @@ def rotary_tables(nc, keep, work, quarter_square):
     cos_tab = keep.tile([P, SLOTS, HALF], F32)
     sin_tab = keep.tile([P, SLOTS, HALF], F32)
 
-    def finish(table_slots, products, sign):
+    def finish(engine, table_slots, products, sign):
         count = products.shape[1]
-        nc.vector.tensor_scalar(
+        engine.tensor_scalar(
             out=table_slots.rearrange("p s (j e) -> p s j e", e=2),
             in0=products.unsqueeze(3).to_broadcast([P, count, FREQS, 2]),
             scalar1=8.0 * sign, scalar2=sign, op0=ALU.mult, op1=ALU.add,
         )
 
-    finish(cos_tab[:], product[:, 0], 1.0)
-    finish(sin_tab[:, 0:BLOCKS], product[:, 1, 0:BLOCKS], -1.0)
-    finish(sin_tab[:, BLOCKS:SLOTS], product[:, 1, BLOCKS:SLOTS], 1.0)
+    finish(nc.gpsimd, cos_tab[:], product[:, 0], 1.0)
+    finish(nc.vector, sin_tab[:, 0:BLOCKS], product[:, 1, 0:BLOCKS], -1.0)
+    finish(nc.vector, sin_tab[:, BLOCKS:SLOTS], product[:, 1, BLOCKS:SLOTS], 1.0)
     return cos_tab, sin_tab
 
 
-def regroup_weights(nc, work, raw):
-    groupeds = []
-    for qk, copy in ((0, nc.scalar.copy), (1, nc.vector.tensor_copy)):
-        grouped = work.tile([P, INNER, PACK], BF16, align_bytes=64, tag="w_grouped%d" % qk)
-        copy(out=grouped[:], in_=raw[:, :, qk * INNER : (qk + 1) * INNER].rearrange("p t n -> p n t"))
-        groupeds.append(grouped)
-    return groupeds
-
-
-def regroup_plain(nc, raw, plain_grouped):
-    for head in range(2 * HEADS):
+def regroup_weights(nc, keep, raw, on_gpsimd):
+    grouped = keep.tile([P, INNER, PACK], BF16, align_bytes=64)
+    columns = raw.rearrange("p t n -> p n t")
+    if on_gpsimd:
         nc.gpsimd.tensor_scalar(
-            out=plain_grouped[:, head * PLAIN : (head + 1) * PLAIN, :],
-            in0=raw[:, :, head * DH + ROT : (head + 1) * DH].rearrange("p t n -> p n t"),
-            scalar1=1.0, scalar2=0.0, op0=ALU.mult, op1=ALU.add,
+            out=grouped[:], in0=columns, scalar1=1.0, scalar2=0.0, op0=ALU.mult, op1=ALU.add
         )
+    else:
+        nc.vector.tensor_copy(out=grouped[:], in_=columns)
+    return grouped
 
 
-def quantise_weights(nc, keep, groupeds, plain_grouped):
-    operands = []
-    for qk in range(2):
-        codes = keep.tile([P, INNER], U32, align_bytes=64, tag="w_codes%d" % qk)
-        scales = keep.tile([P, INNER], U8, align_bytes=64, tag="w_scales%d" % qk)
-        nc.vector.quantize_mx(
-            out=codes[:].bitcast(FP8X4), scales=scales[:],
-            in_=groupeds[qk][:].rearrange("p n t -> p (n t)"),
-        )
-        operands.append((codes, scales))
-    plain_codes = keep.tile([P, DH], U32, align_bytes=64)
-    plain_scales = keep.tile([P, DH], U8, align_bytes=64)
+def quantise_weights(nc, keep, grouped):
+    codes = keep.tile([P, INNER], U32, align_bytes=64)
+    scales = keep.tile([P, INNER], U8, align_bytes=64)
     nc.vector.quantize_mx(
-        out=plain_codes[:].bitcast(FP8X4), scales=plain_scales[:],
-        in_=plain_grouped[:].rearrange("p n t -> p (n t)"),
+        out=codes[:].bitcast(FP8X4), scales=scales[:], in_=grouped[:].rearrange("p n t -> p (n t)")
     )
-    return operands, (plain_codes, plain_scales)
+    return codes, scales
 
 
 def tile_transformerencoderlayer_pa_t_kernel(tc, x_grid, ln_g, ln_b, w_qk, out_0, out_1):
@@ -158,6 +144,7 @@ def tile_transformerencoderlayer_pa_t_kernel(tc, x_grid, ln_g, ln_b, w_qk, out_0
 
     with ExitStack() as ctx:
         keep = ctx.enter_context(tc.tile_pool(name="keep", bufs=1))
+        weights = ctx.enter_context(tc.tile_pool(name="weights", bufs=2))
         work = ctx.enter_context(tc.tile_pool(name="work", bufs=1))
         stats = ctx.enter_context(tc.tile_pool(name="stats", bufs=6))
         stage = ctx.enter_context(tc.tile_pool(name="stage", bufs=3))
@@ -210,14 +197,12 @@ def tile_transformerencoderlayer_pa_t_kernel(tc, x_grid, ln_g, ln_b, w_qk, out_0
         half_t, beta = rotary_factors(nc, work)
         ident = keep.tile([P, P], F32)
         masks.make_identity(nc, ident[:])
-        plain_grouped = work.tile([P, DH, PACK], BF16, align_bytes=64)
-        nc.gpsimd.memset(plain_grouped[:, 2 * HEADS * PLAIN : DH, :], 0.0)
         eighth_sin = work.tile([P, 2, SLOTS, FREQS], F32)
         eighth_square = work.tile([P, 2, SLOTS, FREQS], F32)
         quarter_square = work.tile([P, 2, SLOTS, FREQS], F32)
 
         discard = keep.tile([P, D], BF16)
-        means, variances, rstds, shifts = {}, {}, {}, {}
+        moment_tiles, means, variances, rstds, shifts = {}, {}, {}, {}, {}
         z_tiles, zt_banks, plane_tiles, xn_grouped, xn_operands = {}, {}, {}, {}, {}
         u_banks, plain_banks, y_tiles, partner_tiles = {}, {}, {}, {}
 
@@ -237,7 +222,10 @@ def tile_transformerencoderlayer_pa_t_kernel(tc, x_grid, ln_g, ln_b, w_qk, out_0
                 raw = stats.tile([P, 6], F32, tag="bn%d" % s)
                 nc.vector.bn_stats(out=raw[:], in_=x_sb[:, g, s])
                 nc.vector.bn_aggr(out=moments[:, s], in_=raw[:])
-            means[g], variances[g] = moments[:, :, 0], moments[:, :, 1]
+            moment_tiles[g] = moments
+            for s in range(GROUP):
+                means[(g, s)] = (moments[:, s, 0:1], -1.0)
+                variances[(g, s)] = (moments[:, s, 1:2], 1.0)
 
         def measure_first(g):
             moments = stats.tile([P, 2], F32, name="first_moments")
@@ -271,7 +259,7 @@ def tile_transformerencoderlayer_pa_t_kernel(tc, x_grid, ln_g, ln_b, w_qk, out_0
             rstds[g] = [rstd[:, s : s + 1] for s in range(GROUP)]
 
         def power_rstd(g):
-            mean, variance = means[g], variances[g]
+            mean, variance = moment_tiles[g][:, :, 0], moment_tiles[g][:, :, 1]
             var_eps = stats.tile([P, GROUP], F32)
             nc.gpsimd.tensor_scalar(
                 out=var_eps[:], in0=variance, scalar1=1.0, scalar2=EPS, op0=ALU.mult, op1=ALU.add
@@ -292,7 +280,7 @@ def tile_transformerencoderlayer_pa_t_kernel(tc, x_grid, ln_g, ln_b, w_qk, out_0
                 z_tiles[g] = stage.tile([P, GROUP, D], F32, name="z")
             out = z_tiles[g][:, s].rearrange("p (t m) -> p t m", t=PACK)
             x = x_sb[:, g, s].rearrange("p (m t) -> p t m", t=PACK)
-            if s == 0:
+            if s == 0 and g < LATE:
                 nc.gpsimd.tensor_scalar(
                     out=out, in0=x, scalar1=rstds[g][s], scalar2=shifts[g][s], op0=ALU.mult, op1=ALU.add
                 )
@@ -343,23 +331,25 @@ def tile_transformerencoderlayer_pa_t_kernel(tc, x_grid, ln_g, ln_b, w_qk, out_0
         def project(g, s):
             codes, scales = xn_operands[g]
             tokens = slice(s * P, (s + 1) * P)
-            if s == 0:
-                plain_banks[g] = plain_psum.tile([P, GROUP, DH], F32, name="plain")
-            for qk in range(2):
-                u = u_psum.tile([P, INNER], F32)
+
+            def multiply(out, qk, columns):
+                w_codes, w_scales = w_operands[qk]
                 nc.tensor.matmul_mx(
-                    out=u[:],
+                    out=out,
                     lhsT=codes[:, tokens].bitcast(FP8X4), lhsT_scale=scales[:, tokens],
-                    rhs=w_operands[qk][0][:].bitcast(FP8X4), rhs_scale=w_operands[qk][1][:],
+                    rhs=w_codes[:, columns].bitcast(FP8X4), rhs_scale=w_scales[:, columns],
                     start=True, stop=True,
                 )
+
+            for qk in range(2):
+                u = u_psum.tile([P, INNER], F32)
+                multiply(u[:], qk, slice(0, INNER))
                 u_banks[(g, s, qk)] = u
-            nc.tensor.matmul_mx(
-                out=plain_banks[g][:, s],
-                lhsT=codes[:, tokens].bitcast(FP8X4), lhsT_scale=scales[:, tokens],
-                rhs=plain_operand[0][:].bitcast(FP8X4), rhs_scale=plain_operand[1][:],
-                start=True, stop=True,
-            )
+            if s == 0:
+                plain_banks[g] = plain_psum.tile([P, GROUP, 2 * HEADS, WINDOW], F32, name="plain")
+            for head in range(2 * HEADS):
+                end = DH * (head % HEADS + 1)
+                multiply(plain_banks[g][:, s, head], head // HEADS, slice(end - WINDOW, end))
 
         def multiply_by_tables(g, s, qk):
             a, lane = block_and_lane(g)
@@ -393,7 +383,7 @@ def tile_transformerencoderlayer_pa_t_kernel(tc, x_grid, ln_g, ln_b, w_qk, out_0
         def copy_plain(g):
             nc.scalar.copy(
                 out=y_tiles[g][:].rearrange("p q h s c -> p s (q h) c")[:, :, :, ROT:DH],
-                in_=plain_banks[g][:, :, 0 : 2 * HEADS * PLAIN].rearrange("p s (g c) -> p s g c", c=PLAIN),
+                in_=plain_banks[g][:, :, :, WINDOW - PLAIN : WINDOW],
             )
 
         def store(g):
@@ -407,29 +397,30 @@ def tile_transformerencoderlayer_pa_t_kernel(tc, x_grid, ln_g, ln_b, w_qk, out_0
         def exists(g):
             return 0 <= g < GROUPS
 
+        w_grouped = [regroup_weights(nc, weights, w_raw[:, :, 0:INNER], True)]
         measure_whole(0)
         turns = rotary_turns(nc, work, half_t, beta)
-        w_grouped = regroup_weights(nc, work, w_raw)
         for quarter in range(2):
             nc.scalar.activation(
                 out=eighth_sin[:, quarter], in_=turns[:], func=ACT.Sin,
                 scale=math.pi / 4, bias=quarter_back[:, quarter : quarter + 1],
             )
-        nc.scalar.activation(out=eighth_square[:], in_=eighth_sin[:], func=ACT.Square)
         power_rstd(0)
         normalise(0, 0)
         normalise(0, 1)
         transpose(0)
+        nc.scalar.activation(out=eighth_square[:], in_=eighth_sin[:], func=ACT.Square)
         nc.scalar.activation(out=quarter_square[:], in_=eighth_square[:], func=ACT.Square, scale=-2.0, bias=1.0)
         gain = keep.tile([P, PACK], F32)
         nc.gpsimd.tensor_copy(out=gain[:], in_=gain_raw[:])
         bias = keep.tile([P, PACK], F32)
         nc.gpsimd.tensor_copy(out=bias[:], in_=bias_raw[:])
-        regroup_plain(nc, w_raw, plain_grouped)
+        w_grouped.append(regroup_weights(nc, weights, w_raw[:, :, INNER : 2 * INNER], False))
         measure_whole(1)
         power_rstd(1)
-        w_operands, plain_operand = quantise_weights(nc, keep, w_grouped, plain_grouped)
-        cos_tab, sin_tab = rotary_tables(nc, keep, work, quarter_square)
+        w_operands = [quantise_weights(nc, weights, grouped) for grouped in w_grouped]
+        measure_whole(2)
+        measure_whole(3)
 
         for j in range(-2, GROUPS + 1):
             first, later = j + 2, j + 3
@@ -450,23 +441,24 @@ def tile_transformerencoderlayer_pa_t_kernel(tc, x_grid, ln_g, ln_b, w_qk, out_0
                 store(j - 1)
             if exists(first):
                 regroup(first)
-            if exists(later) and j < 0:
-                normalise(later, 0)
-                normalise(later, 1)
             if j == -2:
-                nc.scalar.activation(out=warm[:], in_=eps[:], func=ACT.Abs_reciprocal_sqrt)
-                measure_whole(2)
-                power_rstd(2)
+                normalise(1, 0)
+                normalise(1, 1)
+                cos_tab, sin_tab = rotary_tables(nc, keep, work, quarter_square)
+                table_rstd(2)
+                table_rstd(3)
             if exists(j):
                 multiply_by_tables(j, 0, 0)
                 multiply_by_tables(j, 0, 1)
             if exists(j + 1):
                 quantise(j + 1)
             if j == -1:
-                measure_whole(3)
-                power_rstd(3)
                 measure_first(new)
-            if exists(j + 4) and j + 4 >= WHOLE and j >= 0:
+                finish_statistics(2)
+                finish_statistics(3)
+                normalise(2, 0)
+                normalise(2, 1)
+            if exists(j + 4) and j >= 0:
                 finish_statistics(j + 4)
             if exists(j):
                 add(j, 0)

@@ -81,47 +81,36 @@ def rotary_factors(nc, work):
     return half_t, beta[:].rearrange("p i j -> p (i j)")[:, 0:FREQS]
 
 
-def rotary_turns(nc, work, half_t, beta):
+def rotary_phases(nc, work, half_t, beta):
     shape = [P, SLOTS, FREQS]
-    turns = work.tile([P, SLOTS, FREQS], F32)
+    turns = work.tile(shape, F32)
     nc.vector.tensor_tensor(
         out=turns[:], in0=half_t[:].unsqueeze(2).to_broadcast(shape),
         in1=beta.unsqueeze(1).to_broadcast(shape), op=ALU.mult,
     )
-    return turns
+    whole = work.tile([P, 2, SLOTS, FREQS], I32)
+    phases = work.tile([P, 2, SLOTS, FREQS], F32)
+    for row, ahead in ((0, 0.25), (1, 0.0)):
+        nc.vector.tensor_scalar_add(out=whole[:, row], in0=turns[:], scalar1=ahead)
+    for row, ahead in ((0, 0.25), (1, 0.0)):
+        nc.vector.scalar_tensor_tensor(
+            out=phases[:, row], in0=turns[:], scalar=ahead, in1=whole[:, row], op0=ALU.add, op1=ALU.subtract
+        )
+    return phases
 
 
-def rotary_tables(nc, keep, work, quarter_square):
-    product = work.tile([P, 2, SLOTS, FREQS], F32)
-    nc.vector.scalar_tensor_tensor(
-        out=product[:], in0=quarter_square[:], scalar=-1.0, in1=quarter_square[:], op0=ALU.add, op1=ALU.mult
+def fill_table(nc, table, phases, slots, sign):
+    chosen = phases[:, slots]
+    nc.scalar.activation(
+        out=table[:, slots].rearrange("p s (j e) -> p s j e", e=2),
+        in_=chosen.unsqueeze(3).to_broadcast([P, chosen.shape[1], FREQS, 2]),
+        func=ACT.Sin, scale=2.0 * math.pi * sign,
     )
-    cos_tab = keep.tile([P, SLOTS, HALF], F32)
-    sin_tab = keep.tile([P, SLOTS, HALF], F32)
-
-    def finish(engine, table_slots, products, sign):
-        count = products.shape[1]
-        engine.tensor_scalar(
-            out=table_slots.rearrange("p s (j e) -> p s j e", e=2),
-            in0=products.unsqueeze(3).to_broadcast([P, count, FREQS, 2]),
-            scalar1=8.0 * sign, scalar2=sign, op0=ALU.mult, op1=ALU.add,
-        )
-
-    finish(nc.gpsimd, cos_tab[:], product[:, 0], 1.0)
-    finish(nc.vector, sin_tab[:, 0:BLOCKS], product[:, 1, 0:BLOCKS], -1.0)
-    finish(nc.vector, sin_tab[:, BLOCKS:SLOTS], product[:, 1, BLOCKS:SLOTS], 1.0)
-    return cos_tab, sin_tab
 
 
-def regroup_weights(nc, keep, raw, on_gpsimd):
+def regroup_weights(nc, keep, raw, copy):
     grouped = keep.tile([P, INNER, PACK], BF16, align_bytes=64)
-    columns = raw.rearrange("p t n -> p n t")
-    if on_gpsimd:
-        nc.gpsimd.tensor_scalar(
-            out=grouped[:], in0=columns, scalar1=1.0, scalar2=0.0, op0=ALU.mult, op1=ALU.add
-        )
-    else:
-        nc.vector.tensor_copy(out=grouped[:], in_=columns)
+    copy(out=grouped[:], in_=raw.rearrange("p t n -> p n t"))
     return grouped
 
 
@@ -186,21 +175,11 @@ def tile_transformerencoderlayer_pa_t_kernel(tc, x_grid, ln_g, ln_b, w_qk, out_0
         nc.vector.tensor_scalar(
             out=eps[:], in0=minus_half[:, 0:1], scalar1=0.0, scalar2=EPS, op0=ALU.mult, op1=ALU.add
         )
-        quarter_back = keep.tile([P, 2], F32)
-        for quarter in range(2):
-            nc.vector.tensor_scalar(
-                out=quarter_back[:, quarter : quarter + 1], in0=minus_half[:, 0:1],
-                scalar1=quarter * math.pi / 8, scalar2=0.0, op0=ALU.mult, op1=ALU.add,
-            )
         warm = work.tile([P, 1], F32)
         nc.scalar.activation(out=warm[:], in_=minus_half[:, 0:1], func=ACT.Sin)
         half_t, beta = rotary_factors(nc, work)
         ident = keep.tile([P, P], F32)
         masks.make_identity(nc, ident[:])
-        eighth_sin = work.tile([P, 2, SLOTS, FREQS], F32)
-        eighth_square = work.tile([P, 2, SLOTS, FREQS], F32)
-        quarter_square = work.tile([P, 2, SLOTS, FREQS], F32)
-
         discard = keep.tile([P, D], BF16)
         moment_tiles, means, variances, rstds, shifts = {}, {}, {}, {}, {}
         z_tiles, zt_banks, plane_tiles, xn_grouped, xn_operands = {}, {}, {}, {}, {}
@@ -225,37 +204,33 @@ def tile_transformerencoderlayer_pa_t_kernel(tc, x_grid, ln_g, ln_b, w_qk, out_0
             moment_tiles[g] = moments
             for s in range(GROUP):
                 means[(g, s)] = (moments[:, s, 0:1], -1.0)
-                variances[(g, s)] = (moments[:, s, 1:2], 1.0)
+            variances[g] = moments[:, :, 1]
 
         def measure_first(g):
-            moments = stats.tile([P, 2], F32, name="first_moments")
+            moments = stats.tile([P, 3], F32, name="mean_and_variances")
             raw = stats.tile([P, 6], F32, tag="bn0")
             nc.vector.bn_stats(out=raw[:], in_=x_sb[:, g, 0])
-            nc.vector.bn_aggr(out=moments[:], in_=raw[:])
+            nc.vector.bn_aggr(out=moments[:, 0:2], in_=raw[:])
             means[(g, 0)] = (moments[:, 0:1], -1.0)
-            variances[(g, 0)] = (moments[:, 1:2], 1.0)
+            moment_tiles[g] = moments
 
         def average_second(g):
             neg_mean = stats.tile([P, 1], F32)
             nc.scalar.activation(
-                out=discard[:], in_=x_sb[:, g, 1], func=ACT.Copy, scale=-1.0 / D, accum_out=neg_mean[:]
+                out=discard[:], in_=x_sb[:, g, 1], func=ACT.Copy, scale=-1.0 / D**1.5, accum_out=neg_mean[:]
             )
-            means[(g, 1)] = (neg_mean[:], 1.0)
+            means[(g, 1)] = (neg_mean[:], D**0.5)
 
         def square_second(g):
-            squares = stats.tile([P, 1], F32)
             nc.scalar.activation(
-                out=discard[:], in_=x_sb[:, g, 1], func=ACT.Square, bias=means[(g, 1)][0], accum_out=squares[:]
+                out=discard[:], in_=x_sb[:, g, 1], func=ACT.Square, scale=D**-0.5, bias=means[(g, 1)][0],
+                accum_out=moment_tiles[g][:, 2:3],
             )
-            variances[(g, 1)] = (squares[:], 1.0 / D)
+            variances[g] = moment_tiles[g][:, 1:3]
 
         def table_rstd(g):
             rstd = stats.tile([P, GROUP], F32, name="rstd_s")
-            for s in range(GROUP):
-                variance, scale = variances[(g, s)]
-                nc.scalar.activation(
-                    out=rstd[:, s : s + 1], in_=variance, func=ACT.Abs_reciprocal_sqrt, scale=scale, bias=eps[:]
-                )
+            nc.scalar.activation(out=rstd[:], in_=variances[g], func=ACT.Abs_reciprocal_sqrt, bias=eps[:])
             rstds[g] = [rstd[:, s : s + 1] for s in range(GROUP)]
 
         def power_rstd(g):
@@ -373,11 +348,10 @@ def tile_transformerencoderlayer_pa_t_kernel(tc, x_grid, ln_g, ln_b, w_qk, out_0
                 op=ALU.mult,
             )
 
-        def add(g, s):
-            engine = nc.vector if s == GROUP - 1 and g >= GROUPS - 2 else nc.gpsimd
-            rows = y_tiles[g][:, :, :, s, 0:ROT].rearrange("p q h c -> p (q h) c")
+        def add(g, s, engine, qk=slice(0, 2)):
+            rows = y_tiles[g][:, qk, :, s, 0:ROT].rearrange("p q h c -> p (q h) c")
             engine.tensor_tensor(
-                out=rows, in0=rows, in1=partner_tiles[g][:, :, :, s].rearrange("p q h c -> p (q h) c"), op=ALU.add
+                out=rows, in0=rows, in1=partner_tiles[g][:, qk, :, s].rearrange("p q h c -> p (q h) c"), op=ALU.add
             )
 
         def copy_plain(g):
@@ -397,25 +371,21 @@ def tile_transformerencoderlayer_pa_t_kernel(tc, x_grid, ln_g, ln_b, w_qk, out_0
         def exists(g):
             return 0 <= g < GROUPS
 
-        w_grouped = [regroup_weights(nc, weights, w_raw[:, :, 0:INNER], True)]
+        w_grouped = [regroup_weights(nc, weights, w_raw[:, :, 0:INNER], nc.scalar.copy)]
         measure_whole(0)
-        turns = rotary_turns(nc, work, half_t, beta)
-        for quarter in range(2):
-            nc.scalar.activation(
-                out=eighth_sin[:, quarter], in_=turns[:], func=ACT.Sin,
-                scale=math.pi / 4, bias=quarter_back[:, quarter : quarter + 1],
-            )
+        phases = rotary_phases(nc, work, half_t, beta)
+        cos_tab = keep.tile([P, SLOTS, HALF], F32)
+        sin_tab = keep.tile([P, SLOTS, HALF], F32)
         power_rstd(0)
         normalise(0, 0)
         normalise(0, 1)
         transpose(0)
-        nc.scalar.activation(out=eighth_square[:], in_=eighth_sin[:], func=ACT.Square)
-        nc.scalar.activation(out=quarter_square[:], in_=eighth_square[:], func=ACT.Square, scale=-2.0, bias=1.0)
+        fill_table(nc, cos_tab, phases[:, 0], slice(0, SLOTS), 1.0)
         gain = keep.tile([P, PACK], F32)
         nc.gpsimd.tensor_copy(out=gain[:], in_=gain_raw[:])
         bias = keep.tile([P, PACK], F32)
         nc.gpsimd.tensor_copy(out=bias[:], in_=bias_raw[:])
-        w_grouped.append(regroup_weights(nc, weights, w_raw[:, :, INNER : 2 * INNER], False))
+        w_grouped.append(regroup_weights(nc, weights, w_raw[:, :, INNER : 2 * INNER], nc.vector.tensor_copy))
         measure_whole(1)
         power_rstd(1)
         w_operands = [quantise_weights(nc, weights, grouped) for grouped in w_grouped]
@@ -426,9 +396,13 @@ def tile_transformerencoderlayer_pa_t_kernel(tc, x_grid, ln_g, ln_b, w_qk, out_0
             first, later = j + 2, j + 3
             new = j + 5
             fresh = exists(new) and new >= WHOLE
-            if exists(j - 1):
-                add(j - 1, 1)
-            if fresh and j >= 0:
+            q, k = slice(0, 1), slice(1, 2)
+            if exists(j - 1) and j < GROUPS - 1:
+                add(j - 1, 1, nc.gpsimd)
+            if j == GROUPS - 1:
+                add(j - 1, 1, nc.gpsimd, q)
+                add(j - 1, 1, nc.vector, k)
+            if fresh and j > 0:
                 measure_first(new)
             if exists(later) and j >= 0:
                 normalise(later, 1)
@@ -442,9 +416,10 @@ def tile_transformerencoderlayer_pa_t_kernel(tc, x_grid, ln_g, ln_b, w_qk, out_0
             if exists(first):
                 regroup(first)
             if j == -2:
+                fill_table(nc, sin_tab, phases[:, 1], slice(0, BLOCKS), -1.0)
+                fill_table(nc, sin_tab, phases[:, 1], slice(BLOCKS, SLOTS), 1.0)
                 normalise(1, 0)
                 normalise(1, 1)
-                cos_tab, sin_tab = rotary_tables(nc, keep, work, quarter_square)
                 table_rstd(2)
                 table_rstd(3)
             if exists(j):
@@ -452,21 +427,27 @@ def tile_transformerencoderlayer_pa_t_kernel(tc, x_grid, ln_g, ln_b, w_qk, out_0
                 multiply_by_tables(j, 0, 1)
             if exists(j + 1):
                 quantise(j + 1)
-            if j == -1:
+            if j in (-1, 0):
                 measure_first(new)
+            if j == -1:
                 finish_statistics(2)
                 finish_statistics(3)
                 normalise(2, 0)
                 normalise(2, 1)
             if exists(j + 4) and j >= 0:
                 finish_statistics(j + 4)
-            if exists(j):
-                add(j, 0)
+            if exists(j) and j < GROUPS - 1:
+                add(j, 0, nc.gpsimd)
             if exists(j + 4) and j >= -1:
                 normalise(j + 4, 0)
             if exists(j):
                 multiply_by_tables(j, 1, 0)
                 multiply_by_tables(j, 1, 1)
+            if j == GROUPS - 1:
+                add(j, 0, nc.gpsimd, q)
+                add(j, 0, nc.gpsimd, k)
+                add(j, 1, nc.gpsimd, q)
+                add(j, 1, nc.vector, k)
             if exists(later) and j >= 0:
                 transpose(later)
             if exists(j + 1):

@@ -392,10 +392,17 @@ def tile_transformerencoderlayer_pa_t_kernel(tc, x_grid, ln_g, ln_b, w_qk, out_0
         measure_whole(2)
         measure_whole(3)
 
+        def measure(g, is_shared):
+            if is_shared:
+                measure_first(g)
+            else:
+                measure_whole(g)
+
         for j in range(-2, GROUPS + 1):
             first, later = j + 2, j + 3
             new = j + 5
             fresh = exists(new) and new >= WHOLE
+            shared = fresh and new % 4 < 3
             q, k = slice(0, 1), slice(1, 2)
             if exists(j - 1) and j < GROUPS - 1:
                 add(j - 1, 1, nc.gpsimd)
@@ -403,12 +410,12 @@ def tile_transformerencoderlayer_pa_t_kernel(tc, x_grid, ln_g, ln_b, w_qk, out_0
                 add(j - 1, 1, nc.gpsimd, q)
                 add(j - 1, 1, nc.vector, k)
             if fresh and j > 0:
-                measure_first(new)
+                measure(new, shared)
             if exists(later) and j >= 0:
                 normalise(later, 1)
             if exists(first):
                 scale_and_shift(first)
-            if fresh:
+            if shared:
                 average_second(new)
             if exists(j - 1):
                 copy_plain(j - 1)
@@ -428,7 +435,7 @@ def tile_transformerencoderlayer_pa_t_kernel(tc, x_grid, ln_g, ln_b, w_qk, out_0
             if exists(j + 1):
                 quantise(j + 1)
             if j in (-1, 0):
-                measure_first(new)
+                measure(new, shared)
             if j == -1:
                 finish_statistics(2)
                 finish_statistics(3)
@@ -455,6 +462,7 @@ def tile_transformerencoderlayer_pa_t_kernel(tc, x_grid, ln_g, ln_b, w_qk, out_0
                 project(j + 1, 1)
             if exists(later) and j < 0:
                 transpose(later)
-            if fresh:
+            if shared:
                 square_second(new)
+            if fresh:
                 table_rstd(new)

@@ -33,8 +33,7 @@ LANES = 8
 GROUP = 2
 GROUPS = BLOCKS * LANES // GROUP
 GROUP_TOKENS = GROUP * P
-LATE = 12
-WHOLE = 4
+LATE = 13
 SLOTS = BLOCKS + LANES
 
 FLOPS = 2 * TOKENS * D * 2 * INNER
@@ -108,7 +107,7 @@ def fill_table(nc, table, phases, slots, sign):
     )
 
 
-def regroup_weights(nc, keep, raw, copy):
+def regroup_weights(keep, raw, copy):
     grouped = keep.tile([P, INNER, PACK], BF16, align_bytes=64)
     copy(out=grouped[:], in_=raw.rearrange("p t n -> p n t"))
     return grouped
@@ -160,12 +159,12 @@ def tile_transformerencoderlayer_pa_t_kernel(tc, x_grid, ln_g, ln_b, w_qk, out_0
         w_raw = work.tile([P, PACK, 2 * INNER], BF16)
         w_view = w_qk.rearrange("(p t) n -> p t n", t=PACK)
         load_x(0)
-        for qk in range(2):
-            columns = slice(qk * INNER, (qk + 1) * INNER)
-            nc.sync.dma_start(out=w_raw[:, :, columns], in_=w_view[:, :, columns])
         load_x(1)
         nc.sync.dma_start(out=gain_raw[:], in_=ln_g.rearrange("(p t) -> p t", t=PACK))
         nc.sync.dma_start(out=bias_raw[:], in_=ln_b.rearrange("(p t) -> p t", t=PACK))
+        for qk in range(2):
+            columns = slice(qk * INNER, (qk + 1) * INNER)
+            nc.sync.dma_start(out=w_raw[:, :, columns], in_=w_view[:, :, columns])
         for g in range(2, GROUPS):
             load_x(g)
 
@@ -181,7 +180,7 @@ def tile_transformerencoderlayer_pa_t_kernel(tc, x_grid, ln_g, ln_b, w_qk, out_0
         ident = keep.tile([P, P], F32)
         masks.make_identity(nc, ident[:])
         discard = keep.tile([P, D], BF16)
-        moment_tiles, means, variances, rstds, shifts = {}, {}, {}, {}, {}
+        raw_tiles, moment_tiles, means, variances, rstds, shifts = {}, {}, {}, {}, {}, {}
         z_tiles, zt_banks, plane_tiles, xn_grouped, xn_operands = {}, {}, {}, {}, {}
         u_banks, plain_banks, y_tiles, partner_tiles = {}, {}, {}, {}
 
@@ -200,19 +199,27 @@ def tile_transformerencoderlayer_pa_t_kernel(tc, x_grid, ln_g, ln_b, w_qk, out_0
             for s in range(GROUP):
                 raw = stats.tile([P, 6], F32, tag="bn%d" % s)
                 nc.vector.bn_stats(out=raw[:], in_=x_sb[:, g, s])
-                nc.vector.bn_aggr(out=moments[:, s], in_=raw[:])
+                raw_tiles[(g, s)] = raw
             moment_tiles[g] = moments
             for s in range(GROUP):
                 means[(g, s)] = (moments[:, s, 0:1], -1.0)
             variances[g] = moments[:, :, 1]
 
         def measure_first(g):
-            moments = stats.tile([P, 3], F32, name="mean_and_variances")
+            moment_tiles[g] = stats.tile([P, 3], F32, name="mean_and_variances")
             raw = stats.tile([P, 6], F32, tag="bn0")
             nc.vector.bn_stats(out=raw[:], in_=x_sb[:, g, 0])
-            nc.vector.bn_aggr(out=moments[:, 0:2], in_=raw[:])
-            means[(g, 0)] = (moments[:, 0:1], -1.0)
-            moment_tiles[g] = moments
+            raw_tiles[(g, 0)] = raw
+            means[(g, 0)] = (moment_tiles[g][:, 0:1], -1.0)
+            variances[g] = moment_tiles[g][:, 1:3]
+
+        def aggregate(g):
+            moments = moment_tiles[g]
+            if (g, 1) in raw_tiles:
+                for s in range(GROUP):
+                    nc.vector.bn_aggr(out=moments[:, s], in_=raw_tiles[(g, s)][:])
+            else:
+                nc.vector.bn_aggr(out=moments[:, 0:2], in_=raw_tiles[(g, 0)][:])
 
         def average_second(g):
             neg_mean = stats.tile([P, 1], F32)
@@ -226,7 +233,6 @@ def tile_transformerencoderlayer_pa_t_kernel(tc, x_grid, ln_g, ln_b, w_qk, out_0
                 out=discard[:], in_=x_sb[:, g, 1], func=ACT.Square, scale=D**-0.5, bias=means[(g, 1)][0],
                 accum_out=moment_tiles[g][:, 2:3],
             )
-            variances[g] = moment_tiles[g][:, 1:3]
 
         def table_rstd(g):
             rstd = stats.tile([P, GROUP], F32, name="rstd_s")
@@ -371,82 +377,91 @@ def tile_transformerencoderlayer_pa_t_kernel(tc, x_grid, ln_g, ln_b, w_qk, out_0
         def exists(g):
             return 0 <= g < GROUPS
 
-        w_grouped = [regroup_weights(nc, weights, w_raw[:, :, 0:INNER], nc.scalar.copy)]
+        w_grouped = [regroup_weights(weights, w_raw[:, :, 0:INNER], nc.scalar.copy)]
         measure_whole(0)
-        phases = rotary_phases(nc, work, half_t, beta)
-        cos_tab = keep.tile([P, SLOTS, HALF], F32)
-        sin_tab = keep.tile([P, SLOTS, HALF], F32)
+        aggregate(0)
         power_rstd(0)
         normalise(0, 0)
         normalise(0, 1)
         transpose(0)
-        fill_table(nc, cos_tab, phases[:, 0], slice(0, SLOTS), 1.0)
-        gain = keep.tile([P, PACK], F32)
-        nc.gpsimd.tensor_copy(out=gain[:], in_=gain_raw[:])
-        bias = keep.tile([P, PACK], F32)
-        nc.gpsimd.tensor_copy(out=bias[:], in_=bias_raw[:])
-        w_grouped.append(regroup_weights(nc, weights, w_raw[:, :, INNER : 2 * INNER], nc.vector.tensor_copy))
         measure_whole(1)
+        aggregate(1)
         power_rstd(1)
-        w_operands = [quantise_weights(nc, weights, grouped) for grouped in w_grouped]
+        normalise(1, 0)
+        gain = keep.tile([P, PACK], F32)
+        nc.vector.tensor_copy(out=gain[:], in_=gain_raw[:])
+        bias = keep.tile([P, PACK], F32)
+        nc.vector.tensor_copy(out=bias[:], in_=bias_raw[:])
         measure_whole(2)
+        aggregate(2)
+        scale_and_shift(0)
+        phases = rotary_phases(nc, work, half_t, beta)
+        cos_tab = keep.tile([P, SLOTS, HALF], F32)
+        sin_tab = keep.tile([P, SLOTS, HALF], F32)
+        fill_table(nc, cos_tab, phases[:, 0], slice(0, SLOTS), 1.0)
+        normalise(1, 1)
+        transpose(1)
+        regroup(0)
+        fill_table(nc, sin_tab, phases[:, 1], slice(0, BLOCKS), -1.0)
+        fill_table(nc, sin_tab, phases[:, 1], slice(BLOCKS, SLOTS), 1.0)
+        w_grouped.append(regroup_weights(weights, w_raw[:, :, INNER : 2 * INNER], nc.vector.tensor_copy))
+        w_operands = [quantise_weights(nc, weights, grouped) for grouped in w_grouped]
+        quantise(0)
         measure_whole(3)
+        aggregate(3)
+        project(0, 0)
+        project(0, 1)
+        scale_and_shift(1)
+        table_rstd(2)
+        table_rstd(3)
+        regroup(1)
 
-        def measure(g, is_shared):
-            if is_shared:
-                measure_first(g)
-            else:
-                measure_whole(g)
-
-        for j in range(-2, GROUPS + 1):
+        for j in range(GROUPS + 1):
             first, later = j + 2, j + 3
-            new = j + 5
-            fresh = exists(new) and new >= WHOLE
-            shared = fresh and new % 4 < 3
+            new = j + 4
+            fresh = exists(new)
             q, k = slice(0, 1), slice(1, 2)
             if exists(j - 1) and j < GROUPS - 1:
                 add(j - 1, 1, nc.gpsimd)
             if j == GROUPS - 1:
                 add(j - 1, 1, nc.gpsimd, q)
                 add(j - 1, 1, nc.vector, k)
-            if fresh and j > 0:
-                measure(new, shared)
-            if exists(later) and j >= 0:
-                normalise(later, 1)
-            if exists(first):
-                scale_and_shift(first)
-            if shared:
+            if fresh:
+                measure_first(new)
+            if j == 0:
+                multiply_by_tables(0, 0, 0)
+                finish_statistics(2)
+                normalise(2, 0)
+                normalise(2, 1)
+                transpose(2)
+            if fresh:
                 average_second(new)
             if exists(j - 1):
                 copy_plain(j - 1)
                 store(j - 1)
             if exists(first):
+                scale_and_shift(first)
+            if fresh:
+                square_second(new)
+            if exists(first):
                 regroup(first)
-            if j == -2:
-                fill_table(nc, sin_tab, phases[:, 1], slice(0, BLOCKS), -1.0)
-                fill_table(nc, sin_tab, phases[:, 1], slice(BLOCKS, SLOTS), 1.0)
-                normalise(1, 0)
-                normalise(1, 1)
-                table_rstd(2)
-                table_rstd(3)
-            if exists(j):
+            if exists(j) and j > 0:
                 multiply_by_tables(j, 0, 0)
+            if fresh:
+                aggregate(new)
+            if exists(j):
                 multiply_by_tables(j, 0, 1)
             if exists(j + 1):
                 quantise(j + 1)
-            if j in (-1, 0):
-                measure(new, shared)
-            if j == -1:
-                finish_statistics(2)
-                finish_statistics(3)
-                normalise(2, 0)
-                normalise(2, 1)
-            if exists(j + 4) and j >= 0:
-                finish_statistics(j + 4)
+            if exists(later):
+                finish_statistics(later)
             if exists(j) and j < GROUPS - 1:
                 add(j, 0, nc.gpsimd)
-            if exists(j + 4) and j >= -1:
-                normalise(j + 4, 0)
+            if exists(later):
+                normalise(later, 0)
+                normalise(later, 1)
+            if fresh:
+                table_rstd(new)
             if exists(j):
                 multiply_by_tables(j, 1, 0)
                 multiply_by_tables(j, 1, 1)
@@ -455,14 +470,8 @@ def tile_transformerencoderlayer_pa_t_kernel(tc, x_grid, ln_g, ln_b, w_qk, out_0
                 add(j, 0, nc.gpsimd, k)
                 add(j, 1, nc.gpsimd, q)
                 add(j, 1, nc.vector, k)
-            if exists(later) and j >= 0:
-                transpose(later)
             if exists(j + 1):
                 project(j + 1, 0)
                 project(j + 1, 1)
-            if exists(later) and j < 0:
+            if exists(later):
                 transpose(later)
-            if shared:
-                square_second(new)
-            if fresh:
-                table_rstd(new)

@@ -33,7 +33,7 @@ LANES = 8
 GROUP = 2
 GROUPS = BLOCKS * LANES // GROUP
 GROUP_TOKENS = GROUP * P
-LATE = 13
+LATE = GROUPS - 3
 SLOTS = BLOCKS + LANES
 
 FLOPS = 2 * TOKENS * D * 2 * INNER
@@ -206,7 +206,7 @@ def tile_transformerencoderlayer_pa_t_kernel(tc, x_grid, ln_g, ln_b, w_qk, out_0
             variances[g] = moments[:, :, 1]
 
         def measure_first(g):
-            moment_tiles[g] = stats.tile([P, 3], F32, name="mean_and_variances")
+            moment_tiles[g] = stats.tile([P, 3], F32, name="moments_of_first")
             raw = stats.tile([P, 6], F32, tag="bn0")
             nc.vector.bn_stats(out=raw[:], in_=x_sb[:, g, 0])
             raw_tiles[(g, 0)] = raw
@@ -366,12 +366,13 @@ def tile_transformerencoderlayer_pa_t_kernel(tc, x_grid, ln_g, ln_b, w_qk, out_0
                 in_=plain_banks[g][:, :, :, WINDOW - PLAIN : WINDOW],
             )
 
-        def store(g):
+        def store(g, steps=range(GROUP)):
             a, lane = block_and_lane(g)
+            start, end = steps[0], steps[-1] + 1
             for qk in range(2):
                 nc.sync.dma_start(
-                    out=out_views[qk][:, :, a, lane * DH : (lane + GROUP) * DH],
-                    in_=y_tiles[g][:, qk].rearrange("p h s c -> p h (s c)"),
+                    out=out_views[qk][:, :, a, (lane + start) * DH : (lane + end) * DH],
+                    in_=y_tiles[g][:, qk, :, start:end].rearrange("p h s c -> p h (s c)"),
                 )
 
         def exists(g):
@@ -416,11 +417,10 @@ def tile_transformerencoderlayer_pa_t_kernel(tc, x_grid, ln_g, ln_b, w_qk, out_0
         table_rstd(3)
         regroup(1)
 
-        for j in range(GROUPS + 1):
-            first, later = j + 2, j + 3
-            new = j + 4
+        q, k = slice(0, 1), slice(1, 2)
+        for j in range(GROUPS):
+            first, later, new = j + 2, j + 3, j + 4
             fresh = exists(new)
-            q, k = slice(0, 1), slice(1, 2)
             if exists(j - 1) and j < GROUPS - 1:
                 add(j - 1, 1, nc.gpsimd)
             if j == GROUPS - 1:
@@ -445,31 +445,32 @@ def tile_transformerencoderlayer_pa_t_kernel(tc, x_grid, ln_g, ln_b, w_qk, out_0
                 square_second(new)
             if exists(first):
                 regroup(first)
-            if exists(j) and j > 0:
+            if j > 0:
                 multiply_by_tables(j, 0, 0)
             if fresh:
                 aggregate(new)
-            if exists(j):
-                multiply_by_tables(j, 0, 1)
+            multiply_by_tables(j, 0, 1)
             if exists(j + 1):
                 quantise(j + 1)
             if exists(later):
                 finish_statistics(later)
-            if exists(j) and j < GROUPS - 1:
+            if j < GROUPS - 1:
                 add(j, 0, nc.gpsimd)
             if exists(later):
                 normalise(later, 0)
                 normalise(later, 1)
             if fresh:
                 table_rstd(new)
-            if exists(j):
-                multiply_by_tables(j, 1, 0)
-                multiply_by_tables(j, 1, 1)
+            multiply_by_tables(j, 1, 0)
+            multiply_by_tables(j, 1, 1)
             if j == GROUPS - 1:
                 add(j, 0, nc.gpsimd, q)
                 add(j, 0, nc.gpsimd, k)
+                copy_plain(j)
+                store(j, range(1))
                 add(j, 1, nc.gpsimd, q)
                 add(j, 1, nc.vector, k)
+                store(j, range(1, GROUP))
             if exists(j + 1):
                 project(j + 1, 0)
                 project(j + 1, 1)

import math
from contextlib import ExitStack

import concourse.masks as masks
import concourse.mybir as mybir

F32 = mybir.dt.float32
BF16 = mybir.dt.bfloat16
I32 = mybir.dt.int32
U32 = mybir.dt.uint32
U8 = mybir.dt.uint8
FP8X4 = mybir.dt.float8_e4m3fn_x4
ALU = mybir.AluOpType
ACT = mybir.ActivationFunctionType

P = 128
PACK = 4
D = P * PACK
TOKENS = 4096
GRID = 64
HEADS = 2
DH = 256
INNER = HEADS * DH
ROT = 200
HALF = ROT // 2
FREQS = HALF // 2
PLAIN = DH - ROT
WINDOW = 64
EPS = 1e-5

BLOCKS = 4
LANES = 8
GROUP = 2
GROUPS = BLOCKS * LANES // GROUP
GROUP_TOKENS = GROUP * P
LATE = GROUPS - 3
SLOTS = BLOCKS + LANES

FLOPS = 2 * TOKENS * D * 2 * INNER


def rotary_factors(nc, work):
    part = work.tile([P, 1], I32)
    nc.gpsimd.iota(part[:], pattern=[[0, 1]], base=0, channel_multiplier=1)
    offsets = work.tile([P, SLOTS], I32)
    nc.gpsimd.iota(
        offsets[:, 0:BLOCKS], pattern=[[2 * GRID // BLOCKS, BLOCKS]], base=1 - GRID, channel_multiplier=0
    )
    nc.gpsimd.iota(offsets[:, BLOCKS:SLOTS], pattern=[[2, LANES]], base=1 - GRID, channel_multiplier=0)
    row_base = work.tile([P, 1], I32)
    nc.vector.tensor_scalar(
        out=row_base[:], in0=part[:], scalar1=3, scalar2=1,
        op0=ALU.arith_shift_right, op1=ALU.logical_shift_left,
    )
    col_base = work.tile([P, 1], I32)
    nc.vector.tensor_scalar(
        out=col_base[:], in0=part[:], scalar1=7, scalar2=4,
        op0=ALU.bitwise_and, op1=ALU.logical_shift_left,
    )
    half_t = work.tile([P, SLOTS], F32)
    for slots, base in ((slice(0, BLOCKS), row_base), (slice(BLOCKS, SLOTS), col_base)):
        nc.vector.tensor_scalar(
            out=half_t[:, slots], in0=offsets[:, slots], scalar1=base[:, 0:1],
            scalar2=0.5 / (GRID - 1), op0=ALU.add, op1=ALU.mult,
        )

    ratio = 5.0 ** (1.0 / (FREQS - 1))
    rows = work.tile([P, 2, 8], F32)
    nc.vector.memset(rows[:, :, 0:1], 1.0)
    for have in (1, 2, 4):
        for row, step in ((0, 8), (1, 1)):
            nc.vector.tensor_scalar_mul(
                out=rows[:, row, have : 2 * have], in0=rows[:, row, 0:have], scalar1=ratio ** (step * have)
            )
    beta = work.tile([P, 8, 8], F32)
    nc.vector.tensor_tensor(
        out=beta[:], in0=rows[:, 0].unsqueeze(2).to_broadcast([P, 8, 8]),
        in1=rows[:, 1].unsqueeze(1).to_broadcast([P, 8, 8]), op=ALU.mult,
    )
    return half_t, beta[:].rearrange("p i j -> p (i j)")[:, 0:FREQS]


def rotary_phases(nc, work, half_t, beta):
    shape = [P, SLOTS, FREQS]
    turns = work.tile(shape, F32)
    nc.vector.tensor_tensor(
        out=turns[:], in0=half_t[:].unsqueeze(2).to_broadcast(shape),
        in1=beta.unsqueeze(1).to_broadcast(shape), op=ALU.mult,
    )
    whole = work.tile([P, 2, SLOTS, FREQS], I32)
    phases = work.tile([P, 2, SLOTS, FREQS], F32)
    for row, ahead in ((0, 0.25), (1, 0.0)):
        nc.vector.tensor_scalar_add(out=whole[:, row], in0=turns[:], scalar1=ahead)
    for row, ahead in ((0, 0.25), (1, 0.0)):
        nc.vector.scalar_tensor_tensor(
            out=phases[:, row], in0=turns[:], scalar=ahead, in1=whole[:, row], op0=ALU.add, op1=ALU.subtract
        )
    return phases


def fill_table(nc, table, phases, slots, sign):
    chosen = phases[:, slots]
    nc.scalar.activation(
        out=table[:, slots].rearrange("p s (j e) -> p s j e", e=2),
        in_=chosen.unsqueeze(3).to_broadcast([P, chosen.shape[1], FREQS, 2]),
        func=ACT.Sin, scale=2.0 * math.pi * sign,
    )


def regroup_weights(keep, raw, copy):
    grouped = keep.tile([P, INNER, PACK], BF16, align_bytes=64)
    copy(out=grouped[:], in_=raw.rearrange("p t n -> p n t"))
    return grouped


def quantise_weights(nc, keep, grouped):
    codes = keep.tile([P, INNER], U32, align_bytes=64)
    scales = keep.tile([P, INNER], U8, align_bytes=64)
    nc.vector.quantize_mx(
        out=codes[:].bitcast(FP8X4), scales=scales[:], in_=grouped[:].rearrange("p n t -> p (n t)")
    )
    return codes, scales


def tile_transformerencoderlayer_pa_t_kernel(tc, x_grid, ln_g, ln_b, w_qk, out_0, out_1):
    nc = tc.nc
    x_view = x_grid.rearrange("o (a p l) k -> p (o a) (l k)", a=BLOCKS, p=P, l=LANES)
    out_views = [
        out.rearrange("o h (a p l) c -> p (o h) a (l c)", a=BLOCKS, p=P, l=LANES)
        for out in (out_0, out_1)
    ]

    with ExitStack() as ctx:
        keep = ctx.enter_context(tc.tile_pool(name="keep", bufs=1))
        weights = ctx.enter_context(tc.tile_pool(name="weights", bufs=2))
        work = ctx.enter_context(tc.tile_pool(name="work", bufs=1))
        stats = ctx.enter_context(tc.tile_pool(name="stats", bufs=6))
        stage = ctx.enter_context(tc.tile_pool(name="stage", bufs=3))
        results = ctx.enter_context(tc.tile_pool(name="results", bufs=4))
        zt_psum = ctx.enter_context(tc.psum_pool(name="zt_psum", bufs=2))
        u_psum = ctx.enter_context(tc.psum_pool(name="u_psum", bufs=4))
        plain_psum = ctx.enter_context(tc.psum_pool(name="plain_psum", bufs=2))
        ctx.enter_context(tc.manual_schedule())

        def block_and_lane(g):
            return g // (LANES // GROUP), GROUP * (g % (LANES // GROUP))

        x_sb = keep.tile([P, GROUPS, GROUP, D], BF16)

        def load_x(g):
            a, lane = block_and_lane(g)
            nc.sync.dma_start(
                out=x_sb[:, g].rearrange("p s k -> p (s k)"),
                in_=x_view[:, a, lane * D : (lane + GROUP) * D],
            )

        gain_raw = work.tile([P, PACK], BF16)
        bias_raw = work.tile([P, PACK], BF16)
        w_raw = work.tile([P, PACK, 2 * INNER], BF16)
        w_view = w_qk.rearrange("(p t) n -> p t n", t=PACK)
        load_x(0)
        load_x(1)
        nc.sync.dma_start(out=gain_raw[:], in_=ln_g.rearrange("(p t) -> p t", t=PACK))
        nc.sync.dma_start(out=bias_raw[:], in_=ln_b.rearrange("(p t) -> p t", t=PACK))
        for qk in range(2):
            columns = slice(qk * INNER, (qk + 1) * INNER)
            nc.sync.dma_start(out=w_raw[:, :, columns], in_=w_view[:, :, columns])
        for g in range(2, GROUPS):
            load_x(g)

        minus_half = keep.tile([P, GROUP], F32)
        nc.vector.memset(minus_half[:], -0.5)
        eps = keep.tile([P, 1], F32)
        nc.vector.tensor_scalar(
            out=eps[:], in0=minus_half[:, 0:1], scalar1=0.0, scalar2=EPS, op0=ALU.mult, op1=ALU.add
        )
        warm = work.tile([P, 1], F32)
        nc.scalar.activation(out=warm[:], in_=minus_half[:, 0:1], func=ACT.Sin)
        half_t, beta = rotary_factors(nc, work)
        ident = keep.tile([P, P], F32)
        masks.make_identity(nc, ident[:])
        discard = keep.tile([P, D], BF16)
        raw_tiles, moment_tiles, means, variances, rstds, shifts = {}, {}, {}, {}, {}, {}
        z_tiles, zt_banks, plane_tiles, xn_grouped, xn_operands = {}, {}, {}, {}, {}
        u_banks, plain_banks, y_tiles, partner_tiles = {}, {}, {}, {}

        def finish_statistics(g):
            shift = stats.tile([P, GROUP], F32)
            for s in range(GROUP):
                mean, sign = means[(g, s)]
                nc.vector.tensor_scalar(
                    out=shift[:, s : s + 1], in0=mean, scalar1=rstds[g][s], scalar2=sign,
                    op0=ALU.mult, op1=ALU.mult,
                )
            shifts[g] = [shift[:, s : s + 1] for s in range(GROUP)]

        def measure_whole(g):
            moments = stats.tile([P, GROUP, 2], F32)
            for s in range(GROUP):
                raw = stats.tile([P, 6], F32, tag="bn%d" % s)
                nc.vector.bn_stats(out=raw[:], in_=x_sb[:, g, s])
                raw_tiles[(g, s)] = raw
            moment_tiles[g] = moments
            for s in range(GROUP):
                means[(g, s)] = (moments[:, s, 0:1], -1.0)
            variances[g] = moments[:, :, 1]

        def measure_first(g):
            moment_tiles[g] = stats.tile([P, 3], F32, name="moments_of_first")
            raw = stats.tile([P, 6], F32, tag="bn0")
            nc.vector.bn_stats(out=raw[:], in_=x_sb[:, g, 0])
            raw_tiles[(g, 0)] = raw
            means[(g, 0)] = (moment_tiles[g][:, 0:1], -1.0)
            variances[g] = moment_tiles[g][:, 1:3]

        def aggregate(g):
            moments = moment_tiles[g]
            if (g, 1) in raw_tiles:
                for s in range(GROUP):
                    nc.vector.bn_aggr(out=moments[:, s], in_=raw_tiles[(g, s)][:])
            else:
                nc.vector.bn_aggr(out=moments[:, 0:2], in_=raw_tiles[(g, 0)][:])

        def average_second(g):
            neg_mean = stats.tile([P, 1], F32)
            nc.scalar.activation(
                out=discard[:], in_=x_sb[:, g, 1], func=ACT.Copy, scale=-1.0 / D**1.5, accum_out=neg_mean[:]
            )
            means[(g, 1)] = (neg_mean[:], D**0.5)

        def square_second(g):
            nc.scalar.activation(
                out=discard[:], in_=x_sb[:, g, 1], func=ACT.Square, scale=D**-0.5, bias=means[(g, 1)][0],
                accum_out=moment_tiles[g][:, 2:3],
            )

        def table_rstd(g):
            rstd = stats.tile([P, GROUP], F32, name="rstd_s")
            nc.scalar.activation(out=rstd[:], in_=variances[g], func=ACT.Abs_reciprocal_sqrt, bias=eps[:])
            rstds[g] = [rstd[:, s : s + 1] for s in range(GROUP)]

        def power_rstd(g):
            mean, variance = moment_tiles[g][:, :, 0], moment_tiles[g][:, :, 1]
            var_eps = stats.tile([P, GROUP], F32)
            nc.gpsimd.tensor_scalar(
                out=var_eps[:], in0=variance, scalar1=1.0, scalar2=EPS, op0=ALU.mult, op1=ALU.add
            )
            rstd = stats.tile([P, GROUP], F32, name="rstd_g")
            nc.gpsimd.tensor_tensor(out=rstd[:], in0=var_eps[:], in1=minus_half[:], op=ALU.pow)
            neg_mean = stats.tile([P, GROUP], F32, name="neg_mean_g")
            nc.gpsimd.tensor_scalar(
                out=neg_mean[:], in0=mean, scalar1=-1.0, scalar2=0.0, op0=ALU.mult, op1=ALU.add
            )
            shift = stats.tile([P, GROUP], F32, name="shift_g")
            nc.gpsimd.tensor_tensor(out=shift[:], in0=neg_mean[:], in1=rstd[:], op=ALU.mult)
            rstds[g] = [rstd[:, s : s + 1] for s in range(GROUP)]
            shifts[g] = [shift[:, s : s + 1] for s in range(GROUP)]

        def normalise(g, s):
            if g not in z_tiles:
                z_tiles[g] = stage.tile([P, GROUP, D], F32, name="z")
            out = z_tiles[g][:, s].rearrange("p (t m) -> p t m", t=PACK)
            x = x_sb[:, g, s].rearrange("p (m t) -> p t m", t=PACK)
            if s == 0 and g < LATE:
                nc.gpsimd.tensor_scalar(
                    out=out, in0=x, scalar1=rstds[g][s], scalar2=shifts[g][s], op0=ALU.mult, op1=ALU.add
                )
            else:
                nc.scalar.activation(out=out, in_=x, func=ACT.Identity, scale=rstds[g][s], bias=shifts[g][s])

        def transpose(g):
            z = z_tiles[g]
            banks = []
            for half in range(2):
                zt = zt_psum.tile([P, 2, GROUP_TOKENS], F32, tag="zt")
                for i in range(2):
                    t = 2 * half + i
                    for s in range(GROUP):
                        nc.tensor.transpose(
                            out=zt[:, i, s * P : (s + 1) * P], in_=z[:, s, t * P : (t + 1) * P],
                            identity=ident[:],
                        )
                banks.append(zt)
            zt_banks[g] = banks

        def scale_and_shift(g):
            planes = stage.tile([P, PACK, GROUP_TOKENS], BF16)
            for t in range(PACK):
                nc.scalar.activation(
                    out=planes[:, t], in_=zt_banks[g][t // 2][:, t % 2], func=ACT.Identity,
                    scale=gain[:, t : t + 1], bias=bias[:, t : t + 1],
                )
            plane_tiles[g] = planes

        def regroup(g):
            grouped = stage.tile([P, GROUP_TOKENS, PACK], BF16, align_bytes=64)
            nc.scalar.copy(
                out=grouped[:].rearrange("p (c i) t -> p c t i", i=4),
                in_=plane_tiles[g][:].rearrange("p t (c i) -> p c t i", i=4),
            )
            xn_grouped[g] = grouped

        def quantise(g):
            codes = stage.tile([P, GROUP_TOKENS], U32, align_bytes=64)
            scales = stage.tile([P, GROUP_TOKENS], U8, align_bytes=64)
            nc.vector.quantize_mx(
                out=codes[:].bitcast(FP8X4), scales=scales[:],
                in_=xn_grouped[g][:].rearrange("p w t -> p (w t)"),
            )
            xn_operands[g] = (codes, scales)

        def project(g, s):
            codes, scales = xn_operands[g]
            tokens = slice(s * P, (s + 1) * P)

            def multiply(out, qk, columns):
                w_codes, w_scales = w_operands[qk]
                nc.tensor.matmul_mx(
                    out=out,
                    lhsT=codes[:, tokens].bitcast(FP8X4), lhsT_scale=scales[:, tokens],
                    rhs=w_codes[:, columns].bitcast(FP8X4), rhs_scale=w_scales[:, columns],
                    start=True, stop=True,
                )

            for qk in range(2):
                u = u_psum.tile([P, INNER], F32)
                multiply(u[:], qk, slice(0, INNER))
                u_banks[(g, s, qk)] = u
            if s == 0:
                plain_banks[g] = plain_psum.tile([P, GROUP, 2 * HEADS, WINDOW], F32, name="plain")
            for head in range(2 * HEADS):
                end = DH * (head % HEADS + 1)
                multiply(plain_banks[g][:, s, head], head // HEADS, slice(end - WINDOW, end))

        def multiply_by_tables(g, s, qk):
            a, lane = block_and_lane(g)
            if s == 0 and qk == 0:
                y_tiles[g] = results.tile([P, 2, HEADS, GROUP, DH], F32, name="y")
                partner_tiles[g] = results.tile([P, 2, HEADS, GROUP, ROT], F32, name="partner")
            both_heads = [P, HEADS, 2, HALF]
            l = lane + s
            slots = slice(a, BLOCKS + l + 1, BLOCKS + l - a)
            u = u_banks[(g, s, qk)][:].rearrange("p (h c) -> p h c", h=HEADS)[:, :, 0:ROT]
            nc.vector.tensor_tensor(
                out=y_tiles[g][:, qk, :, s, 0:ROT].rearrange("p h (f c) -> p h f c", f=2),
                in0=u.rearrange("p h (f c) -> p h f c", f=2),
                in1=cos_tab[:, slots].unsqueeze(1).to_broadcast(both_heads),
                op=ALU.mult,
            )
            nc.vector.tensor_tensor(
                out=partner_tiles[g][:, qk, :, s].rearrange("p h (f i) -> p h f i", f=2),
                in0=u.rearrange("p h (i e) -> p h e i", e=2)[:, :, ::-1, :],
                in1=sin_tab[:, slots].unsqueeze(1).to_broadcast(both_heads),
                op=ALU.mult,
            )

        def add(g, s, engine, qk=slice(0, 2)):
            rows = y_tiles[g][:, qk, :, s, 0:ROT].rearrange("p q h c -> p (q h) c")
            engine.tensor_tensor(
                out=rows, in0=rows, in1=partner_tiles[g][:, qk, :, s].rearrange("p q h c -> p (q h) c"), op=ALU.add
            )

        def copy_plain(g):
            nc.scalar.copy(
                out=y_tiles[g][:].rearrange("p q h s c -> p s (q h) c")[:, :, :, ROT:DH],
                in_=plain_banks[g][:, :, :, WINDOW - PLAIN : WINDOW],
            )

        def store(g, steps=range(GROUP)):
            a, lane = block_and_lane(g)
            start, end = steps[0], steps[-1] + 1
            for qk in range(2):
                nc.sync.dma_start(
                    out=out_views[qk][:, :, a, (lane + start) * DH : (lane + end) * DH],
                    in_=y_tiles[g][:, qk, :, start:end].rearrange("p h s c -> p h (s c)"),
                )

        def exists(g):
            return 0 <= g < GROUPS

        w_grouped = [regroup_weights(weights, w_raw[:, :, 0:INNER], nc.scalar.copy)]
        measure_whole(0)
        aggregate(0)
        power_rstd(0)
        normalise(0, 0)
        normalise(0, 1)
        transpose(0)
        measure_whole(1)
        aggregate(1)
        power_rstd(1)
        normalise(1, 0)
        gain = keep.tile([P, PACK], F32)
        nc.vector.tensor_copy(out=gain[:], in_=gain_raw[:])
        bias = keep.tile([P, PACK], F32)
        nc.vector.tensor_copy(out=bias[:], in_=bias_raw[:])
        measure_whole(2)
        aggregate(2)
        scale_and_shift(0)
        phases = rotary_phases(nc, work, half_t, beta)
        cos_tab = keep.tile([P, SLOTS, HALF], F32)
        sin_tab = keep.tile([P, SLOTS, HALF], F32)
        fill_table(nc, cos_tab, phases[:, 0], slice(0, SLOTS), 1.0)
        normalise(1, 1)
        transpose(1)
        regroup(0)
        fill_table(nc, sin_tab, phases[:, 1], slice(0, BLOCKS), -1.0)
        fill_table(nc, sin_tab, phases[:, 1], slice(BLOCKS, SLOTS), 1.0)
        w_grouped.append(regroup_weights(weights, w_raw[:, :, INNER : 2 * INNER], nc.vector.tensor_copy))
        w_operands = [quantise_weights(nc, weights, grouped) for grouped in w_grouped]
        quantise(0)
        measure_whole(3)
        aggregate(3)
        project(0, 0)
        project(0, 1)
        scale_and_shift(1)
        table_rstd(2)
        table_rstd(3)
        regroup(1)

        q, k = slice(0, 1), slice(1, 2)
        for j in range(GROUPS):
            first, later, new = j + 2, j + 3, j + 4
            fresh = exists(new)
            if exists(j - 1) and j < GROUPS - 1:
                add(j - 1, 1, nc.gpsimd)
            if j == GROUPS - 1:
                add(j - 1, 1, nc.gpsimd, q)
                add(j - 1, 1, nc.vector, k)
            if fresh:
                measure_first(new)
            if j == 0:
                multiply_by_tables(0, 0, 0)
                finish_statistics(2)
                normalise(2, 0)
                normalise(2, 1)
                transpose(2)
            if fresh:
                average_second(new)
            if exists(j - 1):
                copy_plain(j - 1)
                store(j - 1)
            if exists(first):
                scale_and_shift(first)
            if fresh:
                square_second(new)
            if exists(first):
                regroup(first)
            if j > 0:
                multiply_by_tables(j, 0, 0)
            if fresh:
                aggregate(new)
            multiply_by_tables(j, 0, 1)
            if exists(j + 1):
                quantise(j + 1)
            if exists(later):
                finish_statistics(later)
            if j < GROUPS - 1:
                add(j, 0, nc.gpsimd)
            if exists(later):
                normalise(later, 0)
                normalise(later, 1)
            if fresh:
                table_rstd(new)
            multiply_by_tables(j, 1, 0)
            multiply_by_tables(j, 1, 1)
            if j == GROUPS - 1:
                add(j, 0, nc.gpsimd, q)
                add(j, 0, nc.gpsimd, k)
                copy_plain(j)
                store(j, range(1))
                add(j, 1, nc.gpsimd, q)
                add(j, 1, nc.vector, k)
                store(j, range(1, GROUP))
            if exists(j + 1):
                project(j + 1, 0)
                project(j + 1, 1)
            if exists(later):
                transpose(later)
